import numpy as np
import ml_dtypes


def mxq(x, axis, fmt="e4m3"):
    dtype, down = {"e4m3": (ml_dtypes.float8_e4m3fn, 7), "e5m2": (ml_dtypes.float8_e5m2, 14)}[fmt]
    v = np.moveaxis(np.asarray(x, np.float32).astype(ml_dtypes.bfloat16).astype(np.float64), axis, -1)
    blocks = v.reshape(v.shape[:-1] + (-1, 32))
    amax = np.abs(blocks).max(-1, keepdims=True)
    byte = np.maximum(np.where(amax > 0, np.frexp(amax)[1] - 1 + 127, 0) - down, 1)
    scale = np.exp2(byte - 127.0)
    codes = (blocks / scale).astype(np.float32).astype(dtype).astype(np.float64)
    return np.moveaxis((codes * scale).reshape(v.shape), -1, axis)


WIDE = False


def mx_kscale(k):
    if not WIDE:
        return np.ones(k)
    levels = np.array([20, -20, 10, -10, 0])
    a = np.random.permutation(np.resize(levels, k // 512 * 4)).reshape(k // 512, 4)
    idx = np.arange(k)
    return np.exp2(a[idx // 512, idx % 128 // 32])


BF16 = ml_dtypes.bfloat16


def bf(x):
    return np.asarray(x, np.float32).astype(BF16)


def f64(x):
    return np.asarray(x).astype(np.float64)


B, C, O, H, W, KT = 2, 512, 512, 64, 72, 7

OFFSETS = ((0, 0), (-1, 0), (1, 0), (0, -1), (0, 1))


def setup_inputs():
    u = mx_kscale(O)
    x = np.random.standard_normal((B, C, H, W))
    w = np.random.standard_normal((len(OFFSETS), C, KT, KT)) * 2.0
    conv_w = np.random.standard_normal((O, C)) / np.sqrt(C) / u[:, None]
    conv_b = np.random.standard_normal(O) * 0.3 / u
    g = np.random.standard_normal((B, O, H, W)) * np.exp2(np.random.randint(-12, 1, (B, 1, H, W))) * 8.0 * u[None, :, None, None]
    return {"x": bf(x), "w": bf(w), "conv_w": bf(conv_w), "conv_b": bf(conv_b), "grad_out": bf(g)}


def tile_weights(w, hh, ww):
    k = w.shape[-1]
    return np.tile(w, (1, 1, hh // k + 1, ww // k + 1))[:, :, :hh, :ww]


def attention(x, wpos):
    hh, ww = x.shape[2], x.shape[3]
    xh = np.pad(x, ((0, 0), (0, 0), (1, 1), (1, 1)))
    a = np.zeros_like(x)
    for n, (dh, dw) in enumerate(OFFSETS):
        a = a + wpos[n][None] * xh[:, :, 1 + dh:1 + dh + hh, 1 + dw:1 + dw + ww]
    e = np.exp(a - a.max(axis=1, keepdims=True))
    return e / e.sum(axis=1, keepdims=True)


def reference(x, w, conv_w, conv_b, grad_out):
    x, w, conv_w, g = f64(x), f64(w), f64(conv_w), f64(grad_out)
    nb_, nc_, hh, ww = x.shape
    g1 = np.matmul(mxq(conv_w, 0, "e4m3").T, mxq(g, 1, "e5m2").reshape(nb_, -1, hh * ww))
    g1 = g1.reshape(nb_, nc_, hh, ww)
    wpos = tile_weights(w, hh, ww)
    att = attention(x, wpos)
    t = g1 * x
    da = att * (t - (att * t).sum(axis=1, keepdims=True))
    gx = g1 * (1.0 + att)
    for n, (dh, dw) in enumerate(OFFSETS):
        m = np.pad(wpos[n][None] * da, ((0, 0), (0, 0), (1, 1), (1, 1)))
        gx = gx + m[:, :, 1 - dh:1 - dh + hh, 1 - dw:1 - dw + ww]
    return gx

@@ -1,0 +1,291 @@
+from contextlib import ExitStack
+
+import concourse.mybir as mybir
+from concourse.masks import make_identity
+
+F32 = mybir.dt.float32
+BF16 = mybir.dt.bfloat16
+U32 = mybir.dt.uint32
+U8 = mybir.dt.uint8
+E4X4 = mybir.dt.float8_e4m3fn_x4
+E5X4 = mybir.dt.float8_e5m2_x4
+ALU = mybir.AluOpType
+ACT = mybir.ActivationFunctionType
+AX = mybir.AxisListType
+
+NB, C, O, H, W, KT = 2, 512, 512, 64, 72, 7
+HW = H * W
+P = 128
+NCT = C // P
+BLK = KT * W
+MG = 4
+BW = BLK + 2 * MG
+NBLK = (HW + BLK - 1) // BLK
+OFF = (0, -W, W, -1, 1)
+XPAD = W + 2
+XE = BW + 2 * XPAD
+FLOPS = 2 * O * C * NB * HW
+
+
+def back_moves(k, a, ntile):
+    col = P * a
+    moves = []
+    if a == 0 and k > 0:
+        moves.append((k - 1, "up_prev_bank", 48, 3 * P))
+    moves.append((k, "g1", 0, col))
+    moves.append((k, "ag", 0, col))
+    moves.append((k, "m0", 0, col))
+    if a == 0:
+        moves.append((k, "m3", P - 1, 0))
+        if ntile > 1:
+            moves.append((k, "up_first", P - W, 0))
+    else:
+        moves.append((k, "m3", 0, col - 1))
+        moves.append((k, "m1", 0, col - W))
+        moves.append((k, "prev_m4", 0, col - P + 1))
+        moves.append((k, "prev_m2", 0, col - P + W))
+    if a == 0 and k > 0:
+        moves.append((k, "down_next_bank", P - 48, 0))
+    if a == ntile - 1:
+        moves.append((k, "m4", 1, col))
+        if ntile > 1:
+            moves.append((k, "down_last", W, col))
+    return moves
+
+
+def tile_lablock_t_kernel(tc, x, w, conv_w, conv_b, grad_out, out):
+    nc = tc.nc
+    x_v = x.rearrange("b (ct c) h w -> b c ct (h w)", c=P)
+    g_v = grad_out.rearrange("b (p j) h w -> b p j (h w)", j=4)
+    o_v = out.rearrange("b (ct c) h w -> b c ct (h w)", c=P)
+
+    with ExitStack() as ctx:
+        const = ctx.enter_context(tc.tile_pool(name="const", bufs=1))
+        load = ctx.enter_context(tc.tile_pool(name="load", bufs=3))
+        quant = ctx.enter_context(tc.tile_pool(name="quant", bufs=2))
+        work = ctx.enter_context(tc.tile_pool(name="work", bufs=3))
+        edge = ctx.enter_context(tc.tile_pool(name="edge", bufs=2))
+        small = ctx.enter_context(tc.tile_pool(name="small", bufs=4))
+        store = ctx.enter_context(tc.tile_pool(name="store", bufs=2))
+        psum = ctx.enter_context(tc.psum_pool(name="psum", bufs=1))
+
+        ident_f = const.tile([P, P], F32, name="ident_f")
+        make_identity(nc, ident_f[:])
+        ident_b = const.tile([P, P], BF16, name="ident_b")
+        make_identity(nc, ident_b[:])
+        rot = {0: ident_f}
+        for s in (1, 48, W, P - W, P - 48, P - 1):
+            r_t = const.tile([P, P], F32, name="rot%d" % s)
+            nc.vector.tensor_copy(out=r_t[:, s:P], in_=ident_f[:, 0 : P - s])
+            nc.vector.tensor_copy(out=r_t[:, 0:s], in_=ident_f[:, P - s : P])
+            rot[s] = r_t
+        keep = {}
+        for lo, hi in ((1, P), (0, P - 1), (MG, P), (0, P - MG), (W, P), (MG, MG + W), (0, P - W), (52, 52 + W)):
+            k_t = const.tile([P, 1], F32, name="keep%d_%d" % (lo, hi))
+            nc.vector.tensor_reduce(out=k_t[:], in_=ident_f[:, lo:hi], axis=AX.X, op=ALU.add)
+            keep[(lo, hi)] = k_t
+
+        cw_raw = const.tile([P, 4, C], BF16, name="cw_raw")
+        nc.sync.dma_start(out=cw_raw[:], in_=conv_w.rearrange("(p j) c -> p j c", j=4))
+        cw_grp = const.tile([P, C, 4], BF16, name="cw_grp", align_bytes=64)
+        nc.vector.tensor_copy(out=cw_grp[:], in_=cw_raw[:].rearrange("p j c -> p c j"))
+        cw_q = const.tile([P, C], U32, name="cw_q", align_bytes=64)
+        cw_s = const.tile([P, C], U8, name="cw_s", align_bytes=64)
+        nc.vector.quantize_mx(
+            out=cw_q[:].bitcast(E4X4), scales=cw_s[:], in_=cw_grp[:].rearrange("p c j -> p (c j)")
+        )
+
+        wsm = const.tile([P, 5, NCT, 64], BF16, name="wsm")
+        for n in range(5):
+            nc.scalar.dma_start(out=wsm[:, n, :, 0 : KT * KT], in_=w[n].rearrange("(ct c) r s -> c ct (r s)", c=P))
+        wrow = const.tile([P, 5, NCT, BW], BF16, name="wrow")
+        for n in range(5):
+            for ct in range(NCT):
+                rows = wrow[:, n, ct, MG : MG + BLK].rearrange("c (r j) -> c r j", j=W)
+                src = wsm[:, n, ct, 0 : KT * KT].rearrange("c (r s) -> c r s", s=KT)
+                nc.vector.tensor_copy(
+                    out=rows[:, :, 0:70].rearrange("c r (jb s) -> c r jb s", s=KT),
+                    in_=src.unsqueeze(2).to_broadcast([P, KT, 10, KT]),
+                )
+                nc.vector.tensor_copy(out=rows[:, :, 70:72], in_=src[:, :, 0:2])
+        nc.vector.tensor_copy(out=wrow[:, :, :, 0:MG], in_=wrow[:, :, :, BLK : BLK + MG])
+        nc.vector.tensor_copy(out=wrow[:, :, :, BLK + MG : BW], in_=wrow[:, :, :, MG : 2 * MG])
+        nc.vector.memset(wrow[:, 3, :, MG:BW:W], 0.0)
+        nc.vector.memset(wrow[:, 4, :, MG - 1 : BW : W], 0.0)
+
+        cleared = {(0, 3): (1, P), (3, 4): (0, P - 1), (0, 2): (MG, P), (3, 1): (0, P - MG)}
+        wt = const.tile([P, 4, 5, C], BF16, name="wt")
+        for a in range(4):
+            for n in range(5):
+                wps = psum.tile([P, C], BF16, name="wps", tag="at_ps", bufs=2)
+                for ct in range(NCT):
+                    nc.tensor.transpose(
+                        out=wps[:, ct * P : (ct + 1) * P],
+                        in_=wrow[:, n, ct, P * a : P * a + P],
+                        identity=ident_b[:],
+                    )
+                if (a, n) in cleared:
+                    nc.scalar.activation(
+                        out=wt[:, a, n, :], in_=wps[:], func=ACT.Copy, scale=keep[cleared[(a, n)]][:]
+                    )
+                else:
+                    nc.scalar.copy(out=wt[:, a, n, :], in_=wps[:])
+
+        steps = []
+        for b in range(NB):
+            for k in range(NBLK):
+                ncol = min(BLK, HW - BLK * k)
+                ntile = (MG + ncol + P - 1) // P
+                for a in range(ntile):
+                    steps.append((b, k, a, ntile, back_moves(k, a, ntile)))
+        first = {}
+        last = {}
+        for si, (b, k, a, ntile, moves) in enumerate(steps):
+            for mi, mv in enumerate(moves):
+                if (b, mv[0]) not in first:
+                    first[(b, mv[0])] = (si, mi)
+                last[(b, mv[0])] = (si, mi)
+
+        banks = {}
+        terms = {}
+        xs = None
+        g_q = None
+        g_s = None
+        for si, (b, k, a, ntile, moves) in enumerate(steps):
+            if a == 0:
+                base = BLK * k - MG
+                xs = load.tile([P, NCT, XE], BF16, name="xs")
+                lo = base - XPAD
+                hi = lo + XE
+                clo, chi = max(lo, 0), min(hi, HW)
+                if clo != lo or chi != hi:
+                    nc.gpsimd.memset(xs[:], 0.0)
+                nc.sync.dma_start(out=xs[:, :, clo - lo : chi - lo], in_=x_v[b][:, :, clo:chi])
+                g_raw = load.tile([P, 4, BW], BF16, name="g_raw")
+                lo = base
+                hi = lo + BW
+                clo, chi = max(lo, 0), min(hi, HW)
+                if clo != lo or chi != hi:
+                    nc.gpsimd.memset(g_raw[:], 0.0)
+                nc.sync.dma_start(out=g_raw[:, :, clo - lo : chi - lo], in_=g_v[b][:, :, clo:chi])
+                gw = ntile * P
+                g_grp = quant.tile([P, BW, 4], BF16, name="g_grp", align_bytes=64)
+                nc.scalar.copy(out=g_grp[:, 0:gw, :], in_=g_raw[:, :, 0:gw].rearrange("p j q -> p q j"))
+                g_q = quant.tile([P, BW], U32, name="g_q", align_bytes=64)
+                g_s = quant.tile([P, BW], U8, name="g_s", align_bytes=64)
+                nc.vector.quantize_mx(
+                    out=g_q[:, 0:gw].bitcast(E5X4),
+                    scales=g_s[:, 0:gw],
+                    in_=g_grp[:, 0:gw, :].rearrange("p q j -> p (q j)"),
+                )
+
+            prod = work.tile([P, 5, NCT, P], F32, name="prod")
+            for n in range(5):
+                e0 = P * a + XPAD + OFF[n]
+                nc.vector.tensor_tensor(
+                    out=prod[:, n, :, :],
+                    in0=xs[:, :, e0 : e0 + P],
+                    in1=wrow[:, n, :, P * a : P * a + P],
+                    op=ALU.mult,
+                )
+            at_ps = psum.tile([P, C], F32, name="at_ps", tag="at_ps", bufs=2)
+            for ct in range(NCT):
+                for n in range(5):
+                    nc.tensor.matmul(
+                        out=at_ps[:, ct * P : (ct + 1) * P],
+                        lhsT=prod[:, n, ct, :],
+                        rhs=ident_f[:],
+                        is_transpose=True,
+                        start=(n == 0),
+                        stop=(n == 4),
+                    )
+            xt_ps = psum.tile([P, C], BF16, name="xt_ps")
+            e0 = P * a + XPAD
+            for ct in range(NCT):
+                nc.tensor.transpose(
+                    out=xt_ps[:, ct * P : (ct + 1) * P], in_=xs[:, ct, e0 : e0 + P], identity=ident_b[:]
+                )
+            g1_ps = psum.tile([P, C], F32, name="g1_ps")
+            nc.tensor.matmul_mx(
+                out=g1_ps[:],
+                lhsT=g_q[:, a * P : (a + 1) * P].bitcast(E5X4),
+                lhsT_scale=g_s[:, a * P : (a + 1) * P],
+                rhs=cw_q[:].bitcast(E4X4),
+                rhs_scale=cw_s[:],
+                start=True,
+                stop=True,
+            )
+
+            mx = small.tile([P, 1], F32, name="mx")
+            nc.vector.tensor_reduce(out=mx[:], in_=at_ps[:], axis=AX.X, op=ALU.max)
+            nmx = small.tile([P, 1], F32, name="nmx")
+            nc.vector.tensor_scalar_mul(out=nmx[:], in0=mx[:], scalar1=-1.0)
+            ex = work.tile([P, C], F32, name="ex")
+            ssum = small.tile([P, 1], F32, name="ssum")
+            nc.scalar.activation(out=ex[:], in_=at_ps[:], func=ACT.Exp, bias=nmx[:], scale=1.0, accum_out=ssum[:])
+            rs = small.tile([P, 1], F32, name="rs")
+            nc.vector.reciprocal(out=rs[:], in_=ssum[:])
+            g1 = work.tile([P, C], F32, name="g1")
+            nc.scalar.copy(out=g1[:], in_=g1_ps[:])
+            ag = work.tile([P, C], F32, name="ag")
+            nc.vector.scalar_tensor_tensor(
+                out=ag[:], in0=ex[:], scalar=rs[:], in1=g1_ps[:], op0=ALU.mult, op1=ALU.mult
+            )
+            att_t = work.tile([P, C], F32, name="att_t")
+            rr = small.tile([P, 1], F32, name="rr")
+            nc.vector.scalar_tensor_tensor(
+                out=att_t[:], in0=ag[:], scalar=1.0, in1=xt_ps[:], op0=ALU.mult, op1=ALU.mult, accum_out=rr[:]
+            )
+            nrr = small.tile([P, 1], F32, name="nrr")
+            nc.vector.tensor_scalar(
+                out=nrr[:], in0=rr[:], scalar1=rs[:], scalar2=-1.0, op0=ALU.mult, op1=ALU.mult
+            )
+            da = work.tile([P, C], F32, name="da")
+            nc.vector.scalar_tensor_tensor(
+                out=da[:], in0=ex[:], scalar=nrr[:], in1=att_t[:], op0=ALU.mult, op1=ALU.add
+            )
+            m = work.tile([P, 5, C], F32, name="m")
+            nc.vector.tensor_tensor(
+                out=m[:], in0=da[:].unsqueeze(1).to_broadcast([P, 5, C]), in1=wt[:, a, :, :], op=ALU.mult
+            )
+
+            if "m4" in terms:
+                terms["prev_m4"] = terms["m4"]
+                terms["prev_m2"] = terms["m2"]
+            terms["g1"] = g1[:]
+            terms["ag"] = ag[:]
+            for n in range(5):
+                terms["m%d" % n] = m[:, n, :]
+            for name, n, rows, wanted in (
+                ("up_prev_bank", 1, (MG, MG + W), a == 0 and k > 0),
+                ("up_first", 1, (W, P), a == 0 and ntile > 1),
+                ("down_last", 2, (0, P - W), a == 3),
+                ("down_next_bank", 2, (52, 52 + W), a == 3),
+            ):
+                if wanted:
+                    piece = edge.tile([P, C], F32, name=name)
+                    nc.scalar.activation(out=piece[:], in_=m[:, n, :], func=ACT.Copy, scale=keep[rows][:])
+                    terms[name] = piece[:]
+
+            for mi, (bank, term, s, col) in enumerate(moves):
+                if first[(b, bank)] == (si, mi):
+                    banks[bank] = [
+                        psum.tile([P, C], F32, name="ob%d" % ct, tag="ob%d" % ct) for ct in range(NCT)
+                    ]
+                for ct in range(NCT):
+                    nc.tensor.matmul(
+                        out=banks[bank][ct][:, col : col + P],
+                        lhsT=terms[term][:, ct * P : (ct + 1) * P],
+                        rhs=rot[s][:],
+                        is_transpose=True,
+                        start=(first[(b, bank)] == (si, mi)),
+                        stop=(last[(b, bank)] == (si, mi)),
+                    )
+                if last[(b, bank)] == (si, mi):
+                    ncol = min(BLK, HW - BLK * bank)
+                    osb = store.tile([P, NCT, BLK], F32, name="osb")
+                    for ct in range(NCT):
+                        nc.scalar.copy(out=osb[:, ct, 0:ncol], in_=banks[bank][ct][:, MG : MG + ncol])
+                    nc.sync.dma_start(
+                        out=o_v[b][:, :, BLK * bank : BLK * bank + ncol], in_=osb[:, :, 0:ncol]
+                    )

@@ -148,112 +148,168 @@ def tile_lablock_t_kernel(tc, x, w, conv_w, conv_b, grad_out, out):
 
         banks = {}
         terms = {}
-        xs = None
-        g_q = None
-        g_s = None
+        blk = {}
+        st = {}
+        nstep = len(steps)
+        blocks = [(b, k, ntile) for (b, k, a, ntile, moves) in steps if a == 0]
+        block_of = []
         for si, (b, k, a, ntile, moves) in enumerate(steps):
-            if a == 0:
-                base = BLK * k - MG
-                xs = load.tile([P, NCT, XE], BF16, name="xs")
-                lo = base - XPAD
-                hi = lo + XE
-                clo, chi = max(lo, 0), min(hi, HW)
-                if clo != lo or chi != hi:
-                    nc.gpsimd.memset(xs[:], 0.0)
-                nc.sync.dma_start(out=xs[:, :, clo - lo : chi - lo], in_=x_v[b][:, :, clo:chi])
-                g_raw = load.tile([P, 4, BW], BF16, name="g_raw")
-                lo = base
-                hi = lo + BW
-                clo, chi = max(lo, 0), min(hi, HW)
-                if clo != lo or chi != hi:
-                    nc.gpsimd.memset(g_raw[:], 0.0)
-                nc.sync.dma_start(out=g_raw[:, :, clo - lo : chi - lo], in_=g_v[b][:, :, clo:chi])
-                gw = ntile * P
-                g_grp = quant.tile([P, BW, 4], BF16, name="g_grp", align_bytes=64)
-                nc.scalar.copy(out=g_grp[:, 0:gw, :], in_=g_raw[:, :, 0:gw].rearrange("p j q -> p q j"))
-                g_q = quant.tile([P, BW], U32, name="g_q", align_bytes=64)
-                g_s = quant.tile([P, BW], U8, name="g_s", align_bytes=64)
-                nc.vector.quantize_mx(
-                    out=g_q[:, 0:gw].bitcast(E5X4),
-                    scales=g_s[:, 0:gw],
-                    in_=g_grp[:, 0:gw, :].rearrange("p q j -> p (q j)"),
-                )
+            block_of.append(len([1 for s2 in steps[: si + 1] if s2[2] == 0]) - 1)
 
-            prod = work.tile([P, 5, NCT, P], F32, name="prod")
-            for n in range(5):
-                e0 = P * a + XPAD + OFF[n]
-                nc.vector.tensor_tensor(
-                    out=prod[:, n, :, :],
-                    in0=xs[:, :, e0 : e0 + P],
-                    in1=wrow[:, n, :, P * a : P * a + P],
-                    op=ALU.mult,
-                )
-            at_ps = psum.tile([P, C], F32, name="at_ps", tag="at_ps", bufs=2)
-            for ct in range(NCT):
-                for n in range(5):
+        def load_block(bi):
+            b, k, ntile = blocks[bi]
+            base = BLK * k - MG
+            xs = load.tile([P, NCT, XE], BF16, name="xs")
+            lo = base - XPAD
+            hi = lo + XE
+            clo, chi = max(lo, 0), min(hi, HW)
+            if clo != lo or chi != hi:
+                nc.gpsimd.memset(xs[:], 0.0)
+            nc.sync.dma_start(out=xs[:, :, clo - lo : chi - lo], in_=x_v[b][:, :, clo:chi])
+            g_raw = load.tile([P, 4, BW], BF16, name="g_raw")
+            lo = base
+            hi = lo + BW
+            clo, chi = max(lo, 0), min(hi, HW)
+            if clo != lo or chi != hi:
+                nc.gpsimd.memset(g_raw[:], 0.0)
+            nc.sync.dma_start(out=g_raw[:, :, clo - lo : chi - lo], in_=g_v[b][:, :, clo:chi])
+            blk[bi] = {"xs": xs, "g_raw": g_raw}
+
+        def regroup_block(bi):
+            gw = blocks[bi][2] * P
+            g_grp = quant.tile([P, BW, 4], BF16, name="g_grp", align_bytes=64)
+            nc.scalar.copy(
+                out=g_grp[:, 0:gw, :], in_=blk[bi]["g_raw"][:, :, 0:gw].rearrange("p j q -> p q j")
+            )
+            blk[bi]["g_grp"] = g_grp
+
+        def quantise_block(bi):
+            gw = blocks[bi][2] * P
+            g_q = quant.tile([P, BW], U32, name="g_q", align_bytes=64)
+            g_s = quant.tile([P, BW], U8, name="g_s", align_bytes=64)
+            nc.vector.quantize_mx(
+                out=g_q[:, 0:gw].bitcast(E5X4),
+                scales=g_s[:, 0:gw],
+                in_=blk[bi]["g_grp"][:, 0:gw, :].rearrange("p q j -> p (q j)"),
+            )
+            blk[bi]["g_q"] = g_q
+            blk[bi]["g_s"] = g_s
+
+        def product(si, n, eng):
+            a = steps[si][2]
+            if si not in st:
+                st[si] = {"prod": work.tile([P, 5, NCT, P], F32, name="prod")}
+            e0 = P * a + XPAD + OFF[n]
+            eng.tensor_tensor(
+                out=st[si]["prod"][:, n, :, :],
+                in0=blk[block_of[si]]["xs"][:, :, e0 : e0 + P],
+                in1=wrow[:, n, :, P * a : P * a + P],
+                op=ALU.mult,
+            )
+
+        def turn_products(si, taps, opens, closes):
+            if opens:
+                st[si]["at_ps"] = psum.tile([P, C], F32, name="at_ps", tag="at_ps", bufs=2)
+            for ti, n in enumerate(taps):
+                for ct in range(NCT):
                     nc.tensor.matmul(
-                        out=at_ps[:, ct * P : (ct + 1) * P],
-                        lhsT=prod[:, n, ct, :],
+                        out=st[si]["at_ps"][:, ct * P : (ct + 1) * P],
+                        lhsT=st[si]["prod"][:, n, ct, :],
                         rhs=ident_f[:],
                         is_transpose=True,
-                        start=(n == 0),
-                        stop=(n == 4),
+                        start=(opens and ti == 0 and ct == 0),
+                        stop=(closes and ti == len(taps) - 1 and ct == NCT - 1),
                     )
+
+        def turn_x_and_multiply(si):
+            a = steps[si][2]
+            bl = blk[block_of[si]]
             xt_ps = psum.tile([P, C], BF16, name="xt_ps")
             e0 = P * a + XPAD
             for ct in range(NCT):
                 nc.tensor.transpose(
-                    out=xt_ps[:, ct * P : (ct + 1) * P], in_=xs[:, ct, e0 : e0 + P], identity=ident_b[:]
+                    out=xt_ps[:, ct * P : (ct + 1) * P], in_=bl["xs"][:, ct, e0 : e0 + P], identity=ident_b[:]
                 )
             g1_ps = psum.tile([P, C], F32, name="g1_ps")
             nc.tensor.matmul_mx(
                 out=g1_ps[:],
-                lhsT=g_q[:, a * P : (a + 1) * P].bitcast(E5X4),
-                lhsT_scale=g_s[:, a * P : (a + 1) * P],
+                lhsT=bl["g_q"][:, a * P : (a + 1) * P].bitcast(E5X4),
+                lhsT_scale=bl["g_s"][:, a * P : (a + 1) * P],
                 rhs=cw_q[:].bitcast(E4X4),
                 rhs_scale=cw_s[:],
                 start=True,
                 stop=True,
             )
-
-            mx = small.tile([P, 1], F32, name="mx")
-            nc.vector.tensor_reduce(out=mx[:], in_=at_ps[:], axis=AX.X, op=ALU.max)
-            nmx = small.tile([P, 1], F32, name="nmx")
-            nc.vector.tensor_scalar_mul(out=nmx[:], in0=mx[:], scalar1=-1.0)
-            ex = work.tile([P, C], F32, name="ex")
-            ssum = small.tile([P, 1], F32, name="ssum")
-            nc.scalar.activation(out=ex[:], in_=at_ps[:], func=ACT.Exp, bias=nmx[:], scale=1.0, accum_out=ssum[:])
-            rs = small.tile([P, 1], F32, name="rs")
-            nc.vector.reciprocal(out=rs[:], in_=ssum[:])
             g1 = work.tile([P, C], F32, name="g1")
             nc.scalar.copy(out=g1[:], in_=g1_ps[:])
+            st[si]["xt_ps"] = xt_ps
+            st[si]["g1_ps"] = g1_ps
+            st[si]["g1"] = g1
+
+        def maximum_and_exp(si):
+            s_ = st[si]
+            mx = small.tile([P, 1], F32, name="mx")
+            nc.vector.tensor_reduce(out=mx[:], in_=s_["at_ps"][:], axis=AX.X, op=ALU.max)
+            nmx = small.tile([P, 1], F32, name="nmx")
+            nc.scalar.mul(out=nmx[:], in_=mx[:], mul=-1.0)
+            ex = work.tile([P, C], F32, name="ex")
+            ssum = small.tile([P, 1], F32, name="ssum")
+            nc.scalar.activation(
+                out=ex[:], in_=s_["at_ps"][:], func=ACT.Exp, bias=nmx[:], scale=1.0, accum_out=ssum[:]
+            )
+            s_["ex"] = ex
+            s_["ssum"] = ssum
+
+        def att_times_g1(si):
+            s_ = st[si]
+            rs = small.tile([P, 1], F32, name="rs")
+            nc.vector.reciprocal(out=rs[:], in_=s_["ssum"][:])
             ag = work.tile([P, C], F32, name="ag")
             nc.vector.scalar_tensor_tensor(
-                out=ag[:], in0=ex[:], scalar=rs[:], in1=g1_ps[:], op0=ALU.mult, op1=ALU.mult
+                out=ag[:], in0=s_["ex"][:], scalar=rs[:], in1=s_["g1_ps"][:], op0=ALU.mult, op1=ALU.mult
             )
+            s_["rs"] = rs
+            s_["ag"] = ag
+
+        def att_times_t(si):
+            s_ = st[si]
             att_t = work.tile([P, C], F32, name="att_t")
             rr = small.tile([P, 1], F32, name="rr")
             nc.vector.scalar_tensor_tensor(
-                out=att_t[:], in0=ag[:], scalar=1.0, in1=xt_ps[:], op0=ALU.mult, op1=ALU.mult, accum_out=rr[:]
+                out=att_t[:], in0=s_["ag"][:], scalar=1.0, in1=s_["xt_ps"][:], op0=ALU.mult, op1=ALU.mult,
+                accum_out=rr[:],
             )
+            s_["att_t"] = att_t
+            s_["rr"] = rr
+
+        def minus_r_over_sum(si):
+            s_ = st[si]
             nrr = small.tile([P, 1], F32, name="nrr")
             nc.vector.tensor_scalar(
-                out=nrr[:], in0=rr[:], scalar1=rs[:], scalar2=-1.0, op0=ALU.mult, op1=ALU.mult
+                out=nrr[:], in0=s_["rr"][:], scalar1=s_["rs"][:], scalar2=-1.0, op0=ALU.mult, op1=ALU.mult
             )
+            s_["nrr"] = nrr
+
+        def logit_gradient(si):
+            s_ = st[si]
             da = work.tile([P, C], F32, name="da")
             nc.vector.scalar_tensor_tensor(
-                out=da[:], in0=ex[:], scalar=nrr[:], in1=att_t[:], op0=ALU.mult, op1=ALU.add
+                out=da[:], in0=s_["ex"][:], scalar=s_["nrr"][:], in1=s_["att_t"][:], op0=ALU.mult, op1=ALU.add
             )
+            s_["da"] = da
+
+        def weighted_gradient_and_back(si):
+            b, k, a, ntile, moves = steps[si]
+            s_ = st[si]
             m = work.tile([P, 5, C], F32, name="m")
             nc.vector.tensor_tensor(
-                out=m[:], in0=da[:].unsqueeze(1).to_broadcast([P, 5, C]), in1=wt[:, a, :, :], op=ALU.mult
+                out=m[:], in0=s_["da"][:].unsqueeze(1).to_broadcast([P, 5, C]), in1=wt[:, a, :, :], op=ALU.mult
             )
-
             if "m4" in terms:
                 terms["prev_m4"] = terms["m4"]
                 terms["prev_m2"] = terms["m2"]
-            terms["g1"] = g1[:]
-            terms["ag"] = ag[:]
+            terms["g1"] = s_["g1"][:]
+            terms["ag"] = s_["ag"][:]
             for n in range(5):
                 terms["m%d" % n] = m[:, n, :]
             for name, n, rows, wanted in (
@@ -266,7 +322,6 @@ def tile_lablock_t_kernel(tc, x, w, conv_w, conv_b, grad_out, out):
                     piece = edge.tile([P, C], F32, name=name)
                     nc.scalar.activation(out=piece[:], in_=m[:, n, :], func=ACT.Copy, scale=keep[rows][:])
                     terms[name] = piece[:]
-
             for mi, (bank, term, s, col) in enumerate(moves):
                 if first[(b, bank)] == (si, mi):
                     banks[bank] = [
@@ -289,3 +344,48 @@ def tile_lablock_t_kernel(tc, x, w, conv_w, conv_b, grad_out, out):
                     nc.sync.dma_start(
                         out=o_v[b][:, :, BLK * bank : BLK * bank + ncol], in_=osb[:, :, 0:ncol]
                     )
+
+        load_block(0)
+        load_block(1)
+        regroup_block(0)
+        quantise_block(0)
+        ctx.enter_context(tc.manual_schedule())
+        for i in range(-2, nstep):
+            t0, t1, t2 = i, i + 1, i + 2
+            v0 = 0 <= t0
+            v1 = 0 <= t1 < nstep
+            v2 = t2 < nstep
+            new_block = v0 and steps[t0][2] == 0
+            nxt = block_of[t0] + 1 if v0 else 0
+            if new_block and nxt + 1 < len(blocks):
+                load_block(nxt + 1)
+            if new_block and nxt < len(blocks):
+                regroup_block(nxt)
+            if v2:
+                product(t2, 4, nc.gpsimd)
+            if v0:
+                att_times_g1(t0)
+            if v1:
+                maximum_and_exp(t1)
+            if v0:
+                att_times_t(t0)
+            if v2:
+                product(t2, 0, nc.vector)
+                turn_products(t2, (4, 0), True, False)
+            if v0:
+                minus_r_over_sum(t0)
+            if v2:
+                product(t2, 1, nc.vector)
+                turn_products(t2, (1,), False, False)
+            if new_block and nxt < len(blocks):
+                quantise_block(nxt)
+            if v0:
+                logit_gradient(t0)
+            if v1:
+                turn_x_and_multiply(t1)
+            if v2:
+                product(t2, 2, nc.vector)
+                product(t2, 3, nc.vector)
+                turn_products(t2, (2, 3), False, True)
+            if v0:
+                weighted_gradient_and_back(t0)

@@ -147,9 +147,9 @@ def tile_lablock_t_kernel(tc, x, w, conv_w, conv_b, grad_out, out):
                 last[(b, mv[0])] = (si, mi)
 
         banks = {}
-        terms = {}
         blk = {}
         st = {}
+        mxs = {"bank": None, "last": None}
         nstep = len(steps)
         blocks = [(b, k, ntile) for (b, k, a, ntile, moves) in steps if a == 0]
         block_of = []
@@ -221,6 +221,25 @@ def tile_lablock_t_kernel(tc, x, w, conv_w, conv_b, grad_out, out):
                         stop=(closes and ti == len(taps) - 1 and ct == NCT - 1),
                     )
 
+        def mx_pass(si, target):
+            a = steps[si][2]
+            bl = blk[block_of[si]]
+            nc.tensor.matmul_mx(
+                out=target[:],
+                lhsT=bl["g_q"][:, a * P : (a + 1) * P].bitcast(E5X4),
+                lhsT_scale=bl["g_s"][:, a * P : (a + 1) * P],
+                rhs=cw_q[:].bitcast(E4X4),
+                rhs_scale=cw_s[:],
+                start=True,
+                stop=True,
+            )
+
+        def keep_clock():
+            if mxs["last"] is not None and mxs["last"] + 1 < nstep:
+                if mxs["bank"] is None:
+                    mxs["bank"] = psum.tile([P, C], F32, name="g1_ps")
+                mx_pass(mxs["last"], mxs["bank"])
+
         def turn_x_and_multiply(si):
             a = steps[si][2]
             bl = blk[block_of[si]]
@@ -230,20 +249,14 @@ def tile_lablock_t_kernel(tc, x, w, conv_w, conv_b, grad_out, out):
                 nc.tensor.transpose(
                     out=xt_ps[:, ct * P : (ct + 1) * P], in_=bl["xs"][:, ct, e0 : e0 + P], identity=ident_b[:]
                 )
-            g1_ps = psum.tile([P, C], F32, name="g1_ps")
-            nc.tensor.matmul_mx(
-                out=g1_ps[:],
-                lhsT=bl["g_q"][:, a * P : (a + 1) * P].bitcast(E5X4),
-                lhsT_scale=bl["g_s"][:, a * P : (a + 1) * P],
-                rhs=cw_q[:].bitcast(E4X4),
-                rhs_scale=cw_s[:],
-                start=True,
-                stop=True,
-            )
+            if mxs["bank"] is None:
+                mxs["bank"] = psum.tile([P, C], F32, name="g1_ps")
+            mx_pass(si, mxs["bank"])
             g1 = work.tile([P, C], F32, name="g1")
-            nc.scalar.copy(out=g1[:], in_=g1_ps[:])
+            nc.scalar.copy(out=g1[:], in_=mxs["bank"][:])
+            mxs["bank"] = None
+            mxs["last"] = si
             st[si]["xt_ps"] = xt_ps
-            st[si]["g1_ps"] = g1_ps
             st[si]["g1"] = g1
 
         def maximum_and_exp(si):
@@ -266,7 +279,7 @@ def tile_lablock_t_kernel(tc, x, w, conv_w, conv_b, grad_out, out):
             nc.vector.reciprocal(out=rs[:], in_=s_["ssum"][:])
             ag = work.tile([P, C], F32, name="ag")
             nc.vector.scalar_tensor_tensor(
-                out=ag[:], in0=s_["ex"][:], scalar=rs[:], in1=s_["g1_ps"][:], op0=ALU.mult, op1=ALU.mult
+                out=ag[:], in0=s_["ex"][:], scalar=rs[:], in1=s_["g1"][:], op0=ALU.mult, op1=ALU.mult
             )
             s_["rs"] = rs
             s_["ag"] = ag
@@ -298,16 +311,21 @@ def tile_lablock_t_kernel(tc, x, w, conv_w, conv_b, grad_out, out):
             )
             s_["da"] = da
 
-        def weighted_gradient_and_back(si):
+        def weighted_gradient(si):
             b, k, a, ntile, moves = steps[si]
             s_ = st[si]
             m = work.tile([P, 5, C], F32, name="m")
             nc.vector.tensor_tensor(
                 out=m[:], in0=s_["da"][:].unsqueeze(1).to_broadcast([P, 5, C]), in1=wt[:, a, :, :], op=ALU.mult
             )
-            if "m4" in terms:
-                terms["prev_m4"] = terms["m4"]
-                terms["prev_m2"] = terms["m2"]
+            terms = {}
+            s_["terms"] = terms
+            if si > 0:
+                old = st[si - 1]["terms"]
+                terms["prev_m4"] = old["m4"]
+                terms["prev_m2"] = old["m2"]
+                if "down_next_bank" in old:
+                    terms["down_next_bank"] = old["down_next_bank"]
             terms["g1"] = s_["g1"][:]
             terms["ag"] = s_["ag"][:]
             for n in range(5):
@@ -322,7 +340,13 @@ def tile_lablock_t_kernel(tc, x, w, conv_w, conv_b, grad_out, out):
                     piece = edge.tile([P, C], F32, name=name)
                     nc.scalar.activation(out=piece[:], in_=m[:, n, :], func=ACT.Copy, scale=keep[rows][:])
                     terms[name] = piece[:]
+
+        def back(si, lo, hi):
+            b, k, a, ntile, moves = steps[si]
+            terms = st[si]["terms"]
             for mi, (bank, term, s, col) in enumerate(moves):
+                if mi < lo or mi >= hi:
+                    continue
                 if first[(b, bank)] == (si, mi):
                     banks[bank] = [
                         psum.tile([P, C], F32, name="ob%d" % ct, tag="ob%d" % ct) for ct in range(NCT)
@@ -350,9 +374,10 @@ def tile_lablock_t_kernel(tc, x, w, conv_w, conv_b, grad_out, out):
         regroup_block(0)
         quantise_block(0)
         ctx.enter_context(tc.manual_schedule())
-        for i in range(-2, nstep):
-            t0, t1, t2 = i, i + 1, i + 2
-            v0 = 0 <= t0
+        for i in range(-2, nstep + 1):
+            tb, t0, t1, t2 = i - 1, i, i + 1, i + 2
+            vb = 0 <= tb
+            v0 = 0 <= t0 < nstep
             v1 = 0 <= t1 < nstep
             v2 = t2 < nstep
             new_block = v0 and steps[t0][2] == 0
@@ -363,6 +388,9 @@ def tile_lablock_t_kernel(tc, x, w, conv_w, conv_b, grad_out, out):
                 regroup_block(nxt)
             if v2:
                 product(t2, 4, nc.gpsimd)
+            if vb:
+                back(tb, 0, 3)
+            keep_clock()
             if v0:
                 att_times_g1(t0)
             if v1:
@@ -372,11 +400,14 @@ def tile_lablock_t_kernel(tc, x, w, conv_w, conv_b, grad_out, out):
             if v2:
                 product(t2, 0, nc.vector)
                 turn_products(t2, (4, 0), True, False)
+            keep_clock()
             if v0:
                 minus_r_over_sum(t0)
             if v2:
                 product(t2, 1, nc.vector)
                 turn_products(t2, (1,), False, False)
+            if vb:
+                back(tb, 3, 5)
             if new_block and nxt < len(blocks):
                 quantise_block(nxt)
             if v0:
@@ -387,5 +418,9 @@ def tile_lablock_t_kernel(tc, x, w, conv_w, conv_b, grad_out, out):
                 product(t2, 2, nc.vector)
                 product(t2, 3, nc.vector)
                 turn_products(t2, (2, 3), False, True)
+            keep_clock()
+            if vb:
+                back(tb, 5, 99)
+            keep_clock()
             if v0:
-                weighted_gradient_and_back(t0)
+                weighted_gradient(t0)

@@ -197,8 +197,8 @@ def tile_lablock_t_kernel(tc, x, w, conv_w, conv_b, grad_out, out):
 
         def product(si, n, eng):
             a = steps[si][2]
-            if si not in st:
-                st[si] = {"prod": work.tile([P, 5, NCT, P], F32, name="prod")}
+            if "prod" not in st[si]:
+                st[si]["prod"] = work.tile([P, 5, NCT, P], F32, name="prod")
             e0 = P * a + XPAD + OFF[n]
             eng.tensor_tensor(
                 out=st[si]["prod"][:, n, :, :],
@@ -208,8 +208,8 @@ def tile_lablock_t_kernel(tc, x, w, conv_w, conv_b, grad_out, out):
             )
 
         def turn_products(si, taps, opens, closes):
-            if opens:
-                st[si]["at_ps"] = psum.tile([P, C], F32, name="at_ps", tag="at_ps", bufs=2)
+            if opens and mxs["bank"] is st[si]["at_ps"]:
+                mxs["bank"] = None
             for ti, n in enumerate(taps):
                 for ct in range(NCT):
                     nc.tensor.matmul(
@@ -234,10 +234,15 @@ def tile_lablock_t_kernel(tc, x, w, conv_w, conv_b, grad_out, out):
                 stop=True,
             )
 
+        def reserve_bank(si):
+            if si < nstep:
+                st[si] = {"at_ps": psum.tile([P, C], F32, name="at_ps", tag="at_ps", bufs=2)}
+                mxs["bank"] = st[si]["at_ps"]
+            else:
+                mxs["bank"] = None
+
         def keep_clock():
-            if mxs["last"] is not None and mxs["last"] + 1 < nstep:
-                if mxs["bank"] is None:
-                    mxs["bank"] = psum.tile([P, C], F32, name="g1_ps")
+            if mxs["last"] is not None and mxs["bank"] is not None:
                 mx_pass(mxs["last"], mxs["bank"])
 
         def turn_x_and_multiply(si):
@@ -249,13 +254,12 @@ def tile_lablock_t_kernel(tc, x, w, conv_w, conv_b, grad_out, out):
                 nc.tensor.transpose(
                     out=xt_ps[:, ct * P : (ct + 1) * P], in_=bl["xs"][:, ct, e0 : e0 + P], identity=ident_b[:]
                 )
-            if mxs["bank"] is None:
-                mxs["bank"] = psum.tile([P, C], F32, name="g1_ps")
-            mx_pass(si, mxs["bank"])
+            g1_ps = psum.tile([P, C], F32, name="g1_ps")
+            mx_pass(si, g1_ps)
             g1 = work.tile([P, C], F32, name="g1")
-            nc.scalar.copy(out=g1[:], in_=mxs["bank"][:])
-            mxs["bank"] = None
+            nc.scalar.copy(out=g1[:], in_=g1_ps[:])
             mxs["last"] = si
+            st[si]["g1_ps"] = g1_ps
             st[si]["xt_ps"] = xt_ps
             st[si]["g1"] = g1
 
@@ -279,7 +283,7 @@ def tile_lablock_t_kernel(tc, x, w, conv_w, conv_b, grad_out, out):
             nc.vector.reciprocal(out=rs[:], in_=s_["ssum"][:])
             ag = work.tile([P, C], F32, name="ag")
             nc.vector.scalar_tensor_tensor(
-                out=ag[:], in0=s_["ex"][:], scalar=rs[:], in1=s_["g1"][:], op0=ALU.mult, op1=ALU.mult
+                out=ag[:], in0=s_["ex"][:], scalar=rs[:], in1=s_["g1_ps"][:], op0=ALU.mult, op1=ALU.mult
             )
             s_["rs"] = rs
             s_["ag"] = ag
@@ -374,6 +378,8 @@ def tile_lablock_t_kernel(tc, x, w, conv_w, conv_b, grad_out, out):
         regroup_block(0)
         quantise_block(0)
         ctx.enter_context(tc.manual_schedule())
+        reserve_bank(0)
+        reserve_bank(1)
         for i in range(-2, nstep + 1):
             tb, t0, t1, t2 = i - 1, i, i + 1, i + 2
             vb = 0 <= tb
@@ -395,6 +401,8 @@ def tile_lablock_t_kernel(tc, x, w, conv_w, conv_b, grad_out, out):
                 att_times_g1(t0)
             if v1:
                 maximum_and_exp(t1)
+            if i >= -1:
+                reserve_bank(i + 3)
             if v0:
                 att_times_t(t0)
             if v2:

@@ -25,6 +25,7 @@ OFF = (0, -W, W, -1, 1)
 XPAD = W + 2
 XE = BW + 2 * XPAD
 FLOPS = 2 * O * C * NB * HW
+LEAD_LOAD, LEAD_REGROUP, LEAD_QUANT = 6, 4, 3
 
 
 def back_moves(k, a, ntile):
@@ -62,7 +63,7 @@ def tile_lablock_t_kernel(tc, x, w, conv_w, conv_b, grad_out, out):
     with ExitStack() as ctx:
         const = ctx.enter_context(tc.tile_pool(name="const", bufs=1))
         load = ctx.enter_context(tc.tile_pool(name="load", bufs=3))
-        quant = ctx.enter_context(tc.tile_pool(name="quant", bufs=2))
+        quant = ctx.enter_context(tc.tile_pool(name="quant", bufs=3))
         work = ctx.enter_context(tc.tile_pool(name="work", bufs=3))
         edge = ctx.enter_context(tc.tile_pool(name="edge", bufs=2))
         small = ctx.enter_context(tc.tile_pool(name="small", bufs=4))
@@ -103,11 +104,12 @@ def tile_lablock_t_kernel(tc, x, w, conv_w, conv_b, grad_out, out):
             for ct in range(NCT):
                 rows = wrow[:, n, ct, MG : MG + BLK].rearrange("c (r j) -> c r j", j=W)
                 src = wsm[:, n, ct, 0 : KT * KT].rearrange("c (r s) -> c r s", s=KT)
-                nc.vector.tensor_copy(
+                copy = nc.scalar.copy if n in (2, 3) else nc.vector.tensor_copy
+                copy(
                     out=rows[:, :, 0:70].rearrange("c r (jb s) -> c r jb s", s=KT),
                     in_=src.unsqueeze(2).to_broadcast([P, KT, 10, KT]),
                 )
-                nc.vector.tensor_copy(out=rows[:, :, 70:72], in_=src[:, :, 0:2])
+                copy(out=rows[:, :, 70:72], in_=src[:, :, 0:2])
         nc.vector.tensor_copy(out=wrow[:, :, :, 0:MG], in_=wrow[:, :, :, BLK : BLK + MG])
         nc.vector.tensor_copy(out=wrow[:, :, :, BLK + MG : BW], in_=wrow[:, :, :, MG : 2 * MG])
         nc.vector.memset(wrow[:, 3, :, MG:BW:W], 0.0)
@@ -115,9 +117,10 @@ def tile_lablock_t_kernel(tc, x, w, conv_w, conv_b, grad_out, out):
 
         cleared = {(0, 3): (1, P), (3, 4): (0, P - 1), (0, 2): (MG, P), (3, 1): (0, P - MG)}
         wt = const.tile([P, 4, 5, C], BF16, name="wt")
-        for a in range(4):
+
+        def turn_weights(a):
             for n in range(5):
-                wps = psum.tile([P, C], BF16, name="wps", tag="at_ps", bufs=2)
+                wps = psum.tile([P, C], BF16, name="wps", tag="ob%d" % (n % NCT))
                 for ct in range(NCT):
                     nc.tensor.transpose(
                         out=wps[:, ct * P : (ct + 1) * P],
@@ -128,8 +131,10 @@ def tile_lablock_t_kernel(tc, x, w, conv_w, conv_b, grad_out, out):
                     nc.scalar.activation(
                         out=wt[:, a, n, :], in_=wps[:], func=ACT.Copy, scale=keep[cleared[(a, n)]][:]
                     )
-                else:
+                elif n % 2 == 0:
                     nc.scalar.copy(out=wt[:, a, n, :], in_=wps[:])
+                else:
+                    nc.vector.tensor_copy(out=wt[:, a, n, :], in_=wps[:])
 
         steps = []
         for b in range(NB):
@@ -149,7 +154,6 @@ def tile_lablock_t_kernel(tc, x, w, conv_w, conv_b, grad_out, out):
         banks = {}
         blk = {}
         st = {}
-        mxs = {"bank": None, "last": None}
         nstep = len(steps)
         blocks = [(b, k, ntile) for (b, k, a, ntile, moves) in steps if a == 0]
         block_of = []
@@ -197,8 +201,8 @@ def tile_lablock_t_kernel(tc, x, w, conv_w, conv_b, grad_out, out):
 
         def product(si, n, eng):
             a = steps[si][2]
-            if "prod" not in st[si]:
-                st[si]["prod"] = work.tile([P, 5, NCT, P], F32, name="prod")
+            if si not in st:
+                st[si] = {"prod": work.tile([P, 5, NCT, P], F32, name="prod")}
             e0 = P * a + XPAD + OFF[n]
             eng.tensor_tensor(
                 out=st[si]["prod"][:, n, :, :],
@@ -208,8 +212,8 @@ def tile_lablock_t_kernel(tc, x, w, conv_w, conv_b, grad_out, out):
             )
 
         def turn_products(si, taps, opens, closes):
-            if opens and mxs["bank"] is st[si]["at_ps"]:
-                mxs["bank"] = None
+            if opens:
+                st[si]["at_ps"] = psum.tile([P, C], F32, name="at_ps", tag="at_ps", bufs=2)
             for ti, n in enumerate(taps):
                 for ct in range(NCT):
                     nc.tensor.matmul(
@@ -221,30 +225,6 @@ def tile_lablock_t_kernel(tc, x, w, conv_w, conv_b, grad_out, out):
                         stop=(closes and ti == len(taps) - 1 and ct == NCT - 1),
                     )
 
-        def mx_pass(si, target):
-            a = steps[si][2]
-            bl = blk[block_of[si]]
-            nc.tensor.matmul_mx(
-                out=target[:],
-                lhsT=bl["g_q"][:, a * P : (a + 1) * P].bitcast(E5X4),
-                lhsT_scale=bl["g_s"][:, a * P : (a + 1) * P],
-                rhs=cw_q[:].bitcast(E4X4),
-                rhs_scale=cw_s[:],
-                start=True,
-                stop=True,
-            )
-
-        def reserve_bank(si):
-            if si < nstep:
-                st[si] = {"at_ps": psum.tile([P, C], F32, name="at_ps", tag="at_ps", bufs=2)}
-                mxs["bank"] = st[si]["at_ps"]
-            else:
-                mxs["bank"] = None
-
-        def keep_clock():
-            if mxs["last"] is not None and mxs["bank"] is not None:
-                mx_pass(mxs["last"], mxs["bank"])
-
         def turn_x_and_multiply(si):
             a = steps[si][2]
             bl = blk[block_of[si]]
@@ -255,12 +235,19 @@ def tile_lablock_t_kernel(tc, x, w, conv_w, conv_b, grad_out, out):
                     out=xt_ps[:, ct * P : (ct + 1) * P], in_=bl["xs"][:, ct, e0 : e0 + P], identity=ident_b[:]
                 )
             g1_ps = psum.tile([P, C], F32, name="g1_ps")
-            mx_pass(si, g1_ps)
+            nc.tensor.matmul_mx(
+                out=g1_ps[:],
+                lhsT=bl["g_q"][:, a * P : (a + 1) * P].bitcast(E5X4),
+                lhsT_scale=bl["g_s"][:, a * P : (a + 1) * P],
+                rhs=cw_q[:].bitcast(E4X4),
+                rhs_scale=cw_s[:],
+                start=True,
+                stop=True,
+            )
             g1 = work.tile([P, C], F32, name="g1")
             nc.scalar.copy(out=g1[:], in_=g1_ps[:])
-            mxs["last"] = si
-            st[si]["g1_ps"] = g1_ps
             st[si]["xt_ps"] = xt_ps
+            st[si]["g1_ps"] = g1_ps
             st[si]["g1"] = g1
 
         def maximum_and_exp(si):
@@ -334,15 +321,19 @@ def tile_lablock_t_kernel(tc, x, w, conv_w, conv_b, grad_out, out):
             terms["ag"] = s_["ag"][:]
             for n in range(5):
                 terms["m%d" % n] = m[:, n, :]
+
+        def edge_pieces(si, names):
+            b, k, a, ntile, moves = steps[si]
+            terms = st[si]["terms"]
             for name, n, rows, wanted in (
                 ("up_prev_bank", 1, (MG, MG + W), a == 0 and k > 0),
                 ("up_first", 1, (W, P), a == 0 and ntile > 1),
                 ("down_last", 2, (0, P - W), a == 3),
                 ("down_next_bank", 2, (52, 52 + W), a == 3),
             ):
-                if wanted:
+                if wanted and name in names:
                     piece = edge.tile([P, C], F32, name=name)
-                    nc.scalar.activation(out=piece[:], in_=m[:, n, :], func=ACT.Copy, scale=keep[rows][:])
+                    nc.scalar.activation(out=piece[:], in_=terms["m%d" % n], func=ACT.Copy, scale=keep[rows][:])
                     terms[name] = piece[:]
 
         def back(si, lo, hi):
@@ -373,51 +364,45 @@ def tile_lablock_t_kernel(tc, x, w, conv_w, conv_b, grad_out, out):
                         out=o_v[b][:, :, BLK * bank : BLK * bank + ncol], in_=osb[:, :, 0:ncol]
                     )
 
+        def block_starting_at(si):
+            return block_of[si] if 0 <= si < nstep and steps[si][2] == 0 else None
+
         load_block(0)
-        load_block(1)
         regroup_block(0)
         quantise_block(0)
         ctx.enter_context(tc.manual_schedule())
-        reserve_bank(0)
-        reserve_bank(1)
         for i in range(-2, nstep + 1):
             tb, t0, t1, t2 = i - 1, i, i + 1, i + 2
             vb = 0 <= tb
             v0 = 0 <= t0 < nstep
             v1 = 0 <= t1 < nstep
             v2 = t2 < nstep
-            new_block = v0 and steps[t0][2] == 0
-            nxt = block_of[t0] + 1 if v0 else 0
-            if new_block and nxt + 1 < len(blocks):
-                load_block(nxt + 1)
-            if new_block and nxt < len(blocks):
-                regroup_block(nxt)
+            closing = 1 if (v0 and steps[t0][2] == 0 and steps[t0][1] > 0) else 0
+            closed_b = 1 if (vb and steps[tb][2] == 0 and steps[tb][1] > 0) else 0
+            if block_starting_at(i + LEAD_LOAD) is not None:
+                load_block(block_starting_at(i + LEAD_LOAD))
+            if block_starting_at(i + LEAD_REGROUP) is not None:
+                regroup_block(block_starting_at(i + LEAD_REGROUP))
             if v2:
                 product(t2, 4, nc.gpsimd)
-            if vb:
-                back(tb, 0, 3)
-            keep_clock()
             if v0:
                 att_times_g1(t0)
             if v1:
                 maximum_and_exp(t1)
-            if i >= -1:
-                reserve_bank(i + 3)
             if v0:
                 att_times_t(t0)
             if v2:
                 product(t2, 0, nc.vector)
                 turn_products(t2, (4, 0), True, False)
-            keep_clock()
             if v0:
                 minus_r_over_sum(t0)
             if v2:
                 product(t2, 1, nc.vector)
                 turn_products(t2, (1,), False, False)
             if vb:
-                back(tb, 3, 5)
-            if new_block and nxt < len(blocks):
-                quantise_block(nxt)
+                back(tb, closed_b, 5)
+            if block_starting_at(i + LEAD_QUANT) is not None:
+                quantise_block(block_starting_at(i + LEAD_QUANT))
             if v0:
                 logit_gradient(t0)
             if v1:
@@ -426,9 +411,13 @@ def tile_lablock_t_kernel(tc, x, w, conv_w, conv_b, grad_out, out):
                 product(t2, 2, nc.vector)
                 product(t2, 3, nc.vector)
                 turn_products(t2, (2, 3), False, True)
-            keep_clock()
             if vb:
                 back(tb, 5, 99)
-            keep_clock()
+            if i < 0:
+                turn_weights(2 * (i + 2))
+                turn_weights(2 * (i + 2) + 1)
             if v0:
                 weighted_gradient(t0)
+                edge_pieces(t0, ("up_prev_bank",))
+                back(t0, 0, closing)
+                edge_pieces(t0, ("up_first", "down_last", "down_next_bank"))

@@ -34,7 +34,6 @@ def back_moves(k, a, ntile):
     if a == 0 and k > 0:
         moves.append((k - 1, "up_prev_bank", 48, 3 * P))
     moves.append((k, "g1", 0, col))
-    moves.append((k, "ag", 0, col))
     moves.append((k, "m0", 0, col))
     if a == 0:
         moves.append((k, "m3", P - 1, 0))
@@ -65,7 +64,7 @@ def tile_lablock_t_kernel(tc, x, w, conv_w, conv_b, grad_out, out):
         load = ctx.enter_context(tc.tile_pool(name="load", bufs=3))
         quant = ctx.enter_context(tc.tile_pool(name="quant", bufs=3))
         work = ctx.enter_context(tc.tile_pool(name="work", bufs=3))
-        edge = ctx.enter_context(tc.tile_pool(name="edge", bufs=2))
+        edge = ctx.enter_context(tc.tile_pool(name="edge", bufs=1))
         small = ctx.enter_context(tc.tile_pool(name="small", bufs=4))
         store = ctx.enter_context(tc.tile_pool(name="store", bufs=2))
         psum = ctx.enter_context(tc.psum_pool(name="psum", bufs=1))
@@ -86,9 +85,9 @@ def tile_lablock_t_kernel(tc, x, w, conv_w, conv_b, grad_out, out):
             nc.vector.tensor_reduce(out=k_t[:], in_=ident_f[:, lo:hi], axis=AX.X, op=ALU.add)
             keep[(lo, hi)] = k_t
 
-        cw_raw = const.tile([P, 4, C], BF16, name="cw_raw")
+        cw_raw = load.tile([P, 4, C], BF16, name="cw_raw", tag="g_raw")
         nc.sync.dma_start(out=cw_raw[:], in_=conv_w.rearrange("(p j) c -> p j c", j=4))
-        cw_grp = const.tile([P, C, 4], BF16, name="cw_grp", align_bytes=64)
+        cw_grp = quant.tile([P, C, 4], BF16, name="cw_grp", tag="g_grp", align_bytes=64)
         nc.vector.tensor_copy(out=cw_grp[:], in_=cw_raw[:].rearrange("p j c -> p c j"))
         cw_q = const.tile([P, C], U32, name="cw_q", align_bytes=64)
         cw_s = const.tile([P, C], U8, name="cw_s", align_bytes=64)
@@ -202,7 +201,7 @@ def tile_lablock_t_kernel(tc, x, w, conv_w, conv_b, grad_out, out):
         def product(si, n, eng):
             a = steps[si][2]
             if si not in st:
-                st[si] = {"prod": work.tile([P, 5, NCT, P], F32, name="prod")}
+                st[si] = {"prod": work.tile([P, 5, NCT, P], F32, name="prod", bufs=4)}
             e0 = P * a + XPAD + OFF[n]
             eng.tensor_tensor(
                 out=st[si]["prod"][:, n, :, :],
@@ -277,7 +276,7 @@ def tile_lablock_t_kernel(tc, x, w, conv_w, conv_b, grad_out, out):
 
         def att_times_t(si):
             s_ = st[si]
-            att_t = work.tile([P, C], F32, name="att_t")
+            att_t = work.tile([P, C], F32, name="att_t", bufs=2)
             rr = small.tile([P, 1], F32, name="rr")
             nc.vector.scalar_tensor_tensor(
                 out=att_t[:], in0=s_["ag"][:], scalar=1.0, in1=s_["xt_ps"][:], op0=ALU.mult, op1=ALU.mult,
@@ -296,7 +295,7 @@ def tile_lablock_t_kernel(tc, x, w, conv_w, conv_b, grad_out, out):
 
         def logit_gradient(si):
             s_ = st[si]
-            da = work.tile([P, C], F32, name="da")
+            da = work.tile([P, C], F32, name="da", bufs=2)
             nc.vector.scalar_tensor_tensor(
                 out=da[:], in0=s_["ex"][:], scalar=s_["nrr"][:], in1=s_["att_t"][:], op0=ALU.mult, op1=ALU.add
             )
@@ -317,8 +316,7 @@ def tile_lablock_t_kernel(tc, x, w, conv_w, conv_b, grad_out, out):
                 terms["prev_m2"] = old["m2"]
                 if "down_next_bank" in old:
                     terms["down_next_bank"] = old["down_next_bank"]
-            terms["g1"] = s_["g1"][:]
-            terms["ag"] = s_["ag"][:]
+            terms["g1"] = s_["u"][:]
             for n in range(5):
                 terms["m%d" % n] = m[:, n, :]
 
@@ -371,33 +369,40 @@ def tile_lablock_t_kernel(tc, x, w, conv_w, conv_b, grad_out, out):
         regroup_block(0)
         quantise_block(0)
         ctx.enter_context(tc.manual_schedule())
-        for i in range(-2, nstep + 1):
-            tb, t0, t1, t2 = i - 1, i, i + 1, i + 2
+        for i in range(-3, nstep + 1):
+            tb, t0, t1, t2, t3 = i - 1, i, i + 1, i + 2, i + 3
             vb = 0 <= tb
             v0 = 0 <= t0 < nstep
             v1 = 0 <= t1 < nstep
-            v2 = t2 < nstep
+            v2 = 0 <= t2 < nstep
+            v3 = t3 < nstep
             closing = 1 if (v0 and steps[t0][2] == 0 and steps[t0][1] > 0) else 0
             closed_b = 1 if (vb and steps[tb][2] == 0 and steps[tb][1] > 0) else 0
             if block_starting_at(i + LEAD_LOAD) is not None:
                 load_block(block_starting_at(i + LEAD_LOAD))
             if block_starting_at(i + LEAD_REGROUP) is not None:
                 regroup_block(block_starting_at(i + LEAD_REGROUP))
-            if v2:
-                product(t2, 4, nc.gpsimd)
+            if v3:
+                product(t3, 4, nc.gpsimd)
+                product(t3, 3, nc.gpsimd)
             if v0:
                 att_times_g1(t0)
             if v1:
                 maximum_and_exp(t1)
             if v0:
                 att_times_t(t0)
+            if v3:
+                product(t3, 0, nc.vector)
             if v2:
-                product(t2, 0, nc.vector)
                 turn_products(t2, (4, 0), True, False)
             if v0:
+                u = work.tile([P, C], F32, name="u")
+                nc.gpsimd.tensor_tensor(out=u[:], in0=st[t0]["g1"][:], in1=st[t0]["ag"][:], op=ALU.add)
+                st[t0]["u"] = u
                 minus_r_over_sum(t0)
+            if v3:
+                product(t3, 1, nc.vector)
             if v2:
-                product(t2, 1, nc.vector)
                 turn_products(t2, (1,), False, False)
             if vb:
                 back(tb, closed_b, 5)
@@ -407,13 +412,13 @@ def tile_lablock_t_kernel(tc, x, w, conv_w, conv_b, grad_out, out):
                 logit_gradient(t0)
             if v1:
                 turn_x_and_multiply(t1)
+            if v3:
+                product(t3, 2, nc.vector)
             if v2:
-                product(t2, 2, nc.vector)
-                product(t2, 3, nc.vector)
                 turn_products(t2, (2, 3), False, True)
             if vb:
                 back(tb, 5, 99)
-            if i < 0:
+            if -2 <= i < 0:
                 turn_weights(2 * (i + 2))
                 turn_weights(2 * (i + 2) + 1)
             if v0:

@@ -34,6 +34,7 @@ def back_moves(k, a, ntile):
     if a == 0 and k > 0:
         moves.append((k - 1, "up_prev_bank", 48, 3 * P))
     moves.append((k, "g1", 0, col))
+    moves.append((k, "ag", 0, col))
     moves.append((k, "m0", 0, col))
     if a == 0:
         moves.append((k, "m3", P - 1, 0))
@@ -316,7 +317,8 @@ def tile_lablock_t_kernel(tc, x, w, conv_w, conv_b, grad_out, out):
                 terms["prev_m2"] = old["m2"]
                 if "down_next_bank" in old:
                     terms["down_next_bank"] = old["down_next_bank"]
-            terms["g1"] = s_["u"][:]
+            terms["g1"] = s_["g1"][:]
+            terms["ag"] = s_["ag"][:]
             for n in range(5):
                 terms["m%d" % n] = m[:, n, :]
 
@@ -384,7 +386,6 @@ def tile_lablock_t_kernel(tc, x, w, conv_w, conv_b, grad_out, out):
                 regroup_block(block_starting_at(i + LEAD_REGROUP))
             if v3:
                 product(t3, 4, nc.gpsimd)
-                product(t3, 3, nc.gpsimd)
             if v0:
                 att_times_g1(t0)
             if v1:
@@ -396,9 +397,6 @@ def tile_lablock_t_kernel(tc, x, w, conv_w, conv_b, grad_out, out):
             if v2:
                 turn_products(t2, (4, 0), True, False)
             if v0:
-                u = work.tile([P, C], F32, name="u")
-                nc.gpsimd.tensor_tensor(out=u[:], in0=st[t0]["g1"][:], in1=st[t0]["ag"][:], op=ALU.add)
-                st[t0]["u"] = u
                 minus_r_over_sum(t0)
             if v3:
                 product(t3, 1, nc.vector)
@@ -414,6 +412,7 @@ def tile_lablock_t_kernel(tc, x, w, conv_w, conv_b, grad_out, out):
                 turn_x_and_multiply(t1)
             if v3:
                 product(t3, 2, nc.vector)
+                product(t3, 3, nc.vector)
             if v2:
                 turn_products(t2, (2, 3), False, True)
             if vb:

@@ -264,15 +264,19 @@ def tile_lablock_t_kernel(tc, x, w, conv_w, conv_b, grad_out, out):
             s_["ex"] = ex
             s_["ssum"] = ssum
 
-        def att_times_g1(si):
+        def one_over_sum(si):
             s_ = st[si]
             rs = small.tile([P, 1], F32, name="rs")
             nc.vector.reciprocal(out=rs[:], in_=s_["ssum"][:])
+            s_["rs"] = rs
+
+        def att_times_g1(si):
+            s_ = st[si]
+            rs = s_["rs"]
             ag = work.tile([P, C], F32, name="ag")
             nc.vector.scalar_tensor_tensor(
                 out=ag[:], in0=s_["ex"][:], scalar=rs[:], in1=s_["g1_ps"][:], op0=ALU.mult, op1=ALU.mult
             )
-            s_["rs"] = rs
             s_["ag"] = ag
 
         def att_times_t(si):
@@ -420,6 +424,8 @@ def tile_lablock_t_kernel(tc, x, w, conv_w, conv_b, grad_out, out):
             if -2 <= i < 0:
                 turn_weights(2 * (i + 2))
                 turn_weights(2 * (i + 2) + 1)
+            if v1:
+                one_over_sum(t1)
             if v0:
                 weighted_gradient(t0)
                 edge_pieces(t0, ("up_prev_bank",))

@@ -26,6 +26,7 @@ XPAD = W + 2
 XE = BW + 2 * XPAD
 FLOPS = 2 * O * C * NB * HW
 LEAD_LOAD, LEAD_REGROUP, LEAD_QUANT = 6, 4, 3
+GP_CT = 2
 
 
 def back_moves(k, a, ntile):
@@ -199,15 +200,15 @@ def tile_lablock_t_kernel(tc, x, w, conv_w, conv_b, grad_out, out):
             blk[bi]["g_q"] = g_q
             blk[bi]["g_s"] = g_s
 
-        def product(si, n, eng):
+        def product(si, n, eng, c0=0, c1=NCT):
             a = steps[si][2]
             if si not in st:
                 st[si] = {"prod": work.tile([P, 5, NCT, P], F32, name="prod", bufs=4)}
             e0 = P * a + XPAD + OFF[n]
             eng.tensor_tensor(
-                out=st[si]["prod"][:, n, :, :],
-                in0=blk[block_of[si]]["xs"][:, :, e0 : e0 + P],
-                in1=wrow[:, n, :, P * a : P * a + P],
+                out=st[si]["prod"][:, n, c0:c1, :],
+                in0=blk[block_of[si]]["xs"][:, c0:c1, e0 : e0 + P],
+                in1=wrow[:, n, c0:c1, P * a : P * a + P],
                 op=ALU.mult,
             )
 
@@ -390,6 +391,7 @@ def tile_lablock_t_kernel(tc, x, w, conv_w, conv_b, grad_out, out):
                 regroup_block(block_starting_at(i + LEAD_REGROUP))
             if v3:
                 product(t3, 4, nc.gpsimd)
+                product(t3, 3, nc.gpsimd, 0, GP_CT)
             if v0:
                 att_times_g1(t0)
             if v1:
@@ -416,7 +418,7 @@ def tile_lablock_t_kernel(tc, x, w, conv_w, conv_b, grad_out, out):
                 turn_x_and_multiply(t1)
             if v3:
                 product(t3, 2, nc.vector)
-                product(t3, 3, nc.vector)
+                product(t3, 3, nc.vector, GP_CT, NCT)
             if v2:
                 turn_products(t2, (2, 3), False, True)
             if vb:

@@ -26,7 +26,6 @@ XPAD = W + 2
 XE = BW + 2 * XPAD
 FLOPS = 2 * O * C * NB * HW
 LEAD_LOAD, LEAD_REGROUP, LEAD_QUANT = 6, 4, 3
-GP_CT = 2
 
 
 def back_moves(k, a, ntile):
@@ -120,7 +119,7 @@ def tile_lablock_t_kernel(tc, x, w, conv_w, conv_b, grad_out, out):
         wt = const.tile([P, 4, 5, C], BF16, name="wt")
 
         def turn_weights(a):
-            for n in range(5):
+            for n in range(1, 5):
                 wps = psum.tile([P, C], BF16, name="wps", tag="ob%d" % (n % NCT))
                 for ct in range(NCT):
                     nc.tensor.transpose(
@@ -226,10 +225,21 @@ def tile_lablock_t_kernel(tc, x, w, conv_w, conv_b, grad_out, out):
                         stop=(closes and ti == len(taps) - 1 and ct == NCT - 1),
                     )
 
-        def turn_x_and_multiply(si):
+        def turn_x_and_multiply(si, wi):
+            xt_ps = psum.tile([P, 2 * C], BF16, name="xt_ps")
+            if wi is not None:
+                aw = steps[wi][2]
+                for ct in range(NCT):
+                    nc.tensor.transpose(
+                        out=xt_ps[:, C + ct * P : C + (ct + 1) * P],
+                        in_=wrow[:, 0, ct, P * aw : P * aw + P],
+                        identity=ident_b[:],
+                    )
+                st[wi]["w0_ps"] = xt_ps
+            if si is None:
+                return
             a = steps[si][2]
             bl = blk[block_of[si]]
-            xt_ps = psum.tile([P, C], BF16, name="xt_ps")
             e0 = P * a + XPAD
             for ct in range(NCT):
                 nc.tensor.transpose(
@@ -285,7 +295,7 @@ def tile_lablock_t_kernel(tc, x, w, conv_w, conv_b, grad_out, out):
             att_t = work.tile([P, C], F32, name="att_t", bufs=2)
             rr = small.tile([P, 1], F32, name="rr")
             nc.vector.scalar_tensor_tensor(
-                out=att_t[:], in0=s_["ag"][:], scalar=1.0, in1=s_["xt_ps"][:], op0=ALU.mult, op1=ALU.mult,
+                out=att_t[:], in0=s_["ag"][:], scalar=1.0, in1=s_["xt_ps"][:, 0:C], op0=ALU.mult, op1=ALU.mult,
                 accum_out=rr[:],
             )
             s_["att_t"] = att_t
@@ -312,8 +322,12 @@ def tile_lablock_t_kernel(tc, x, w, conv_w, conv_b, grad_out, out):
             s_ = st[si]
             m = work.tile([P, 5, C], F32, name="m")
             nc.vector.tensor_tensor(
-                out=m[:], in0=s_["da"][:].unsqueeze(1).to_broadcast([P, 5, C]), in1=wt[:, a, :, :], op=ALU.mult
+                out=m[:, 1:5, :],
+                in0=s_["da"][:].unsqueeze(1).to_broadcast([P, 4, C]),
+                in1=wt[:, a, 1:5, :],
+                op=ALU.mult,
             )
+            nc.vector.tensor_tensor(out=m[:, 0, :], in0=s_["da"][:], in1=s_["w0_ps"][:, C : 2 * C], op=ALU.mult)
             terms = {}
             s_["terms"] = terms
             if si > 0:
@@ -391,7 +405,7 @@ def tile_lablock_t_kernel(tc, x, w, conv_w, conv_b, grad_out, out):
                 regroup_block(block_starting_at(i + LEAD_REGROUP))
             if v3:
                 product(t3, 4, nc.gpsimd)
-                product(t3, 3, nc.gpsimd, 0, GP_CT)
+                product(t3, 3, nc.gpsimd)
             if v0:
                 att_times_g1(t0)
             if v1:
@@ -414,11 +428,10 @@ def tile_lablock_t_kernel(tc, x, w, conv_w, conv_b, grad_out, out):
                 quantise_block(block_starting_at(i + LEAD_QUANT))
             if v0:
                 logit_gradient(t0)
-            if v1:
-                turn_x_and_multiply(t1)
+            if v0 or v1:
+                turn_x_and_multiply(t1 if v1 else None, t0 if v0 else None)
             if v3:
                 product(t3, 2, nc.vector)
-                product(t3, 3, nc.vector, GP_CT, NCT)
             if v2:
                 turn_products(t2, (2, 3), False, True)
             if vb:

@@ -17,41 +17,18 @@ NB, C, O, H, W, KT = 2, 512, 512, 64, 72, 7
 HW = H * W
 P = 128
 NCT = C // P
-BLK = KT * W
-MG = 4
-BW = BLK + 2 * MG
-NBLK = (HW + BLK - 1) // BLK
-OFF = (0, -W, W, -1, 1)
-XPAD = W + 2
-XE = BW + 2 * XPAD
+NT = HW // P
+GRP = 4 * P
+PER = KT * W
+WW = PER + P
+TAPS = (1, 0, 2, 3, 4)
+OFF = (-W, 0, W, -1, 1)
+XPAD = 80
+XE = GRP + 2 * XPAD
+RING = 4 * P
+G_TAPS = (2, 3, 4)
+V_TAPS = (0, 1)
 FLOPS = 2 * O * C * NB * HW
-LEAD_LOAD, LEAD_REGROUP, LEAD_QUANT = 6, 4, 3
-
-
-def back_moves(k, a, ntile):
-    col = P * a
-    moves = []
-    if a == 0 and k > 0:
-        moves.append((k - 1, "up_prev_bank", 48, 3 * P))
-    moves.append((k, "g1", 0, col))
-    moves.append((k, "ag", 0, col))
-    moves.append((k, "m0", 0, col))
-    if a == 0:
-        moves.append((k, "m3", P - 1, 0))
-        if ntile > 1:
-            moves.append((k, "up_first", P - W, 0))
-    else:
-        moves.append((k, "m3", 0, col - 1))
-        moves.append((k, "m1", 0, col - W))
-        moves.append((k, "prev_m4", 0, col - P + 1))
-        moves.append((k, "prev_m2", 0, col - P + W))
-    if a == 0 and k > 0:
-        moves.append((k, "down_next_bank", P - 48, 0))
-    if a == ntile - 1:
-        moves.append((k, "m4", 1, col))
-        if ntile > 1:
-            moves.append((k, "down_last", W, col))
-    return moves
 
 
 def tile_lablock_t_kernel(tc, x, w, conv_w, conv_b, grad_out, out):
@@ -65,7 +42,6 @@ def tile_lablock_t_kernel(tc, x, w, conv_w, conv_b, grad_out, out):
         load = ctx.enter_context(tc.tile_pool(name="load", bufs=3))
         quant = ctx.enter_context(tc.tile_pool(name="quant", bufs=3))
         work = ctx.enter_context(tc.tile_pool(name="work", bufs=3))
-        edge = ctx.enter_context(tc.tile_pool(name="edge", bufs=1))
         small = ctx.enter_context(tc.tile_pool(name="small", bufs=4))
         store = ctx.enter_context(tc.tile_pool(name="store", bufs=2))
         psum = ctx.enter_context(tc.psum_pool(name="psum", bufs=1))
@@ -74,21 +50,48 @@ def tile_lablock_t_kernel(tc, x, w, conv_w, conv_b, grad_out, out):
         make_identity(nc, ident_f[:])
         ident_b = const.tile([P, P], BF16, name="ident_b")
         make_identity(nc, ident_b[:])
-        rot = {0: ident_f}
-        for s in (1, 48, W, P - W, P - 48, P - 1):
-            r_t = const.tile([P, P], F32, name="rot%d" % s)
-            nc.vector.tensor_copy(out=r_t[:, s:P], in_=ident_f[:, 0 : P - s])
-            nc.vector.tensor_copy(out=r_t[:, 0:s], in_=ident_f[:, P - s : P])
-            rot[s] = r_t
-        keep = {}
-        for lo, hi in ((1, P), (0, P - 1), (MG, P), (0, P - MG), (W, P), (MG, MG + W), (0, P - W), (52, 52 + W)):
-            k_t = const.tile([P, 1], F32, name="keep%d_%d" % (lo, hi))
-            nc.vector.tensor_reduce(out=k_t[:], in_=ident_f[:, lo:hi], axis=AX.X, op=ALU.add)
-            keep[(lo, hi)] = k_t
 
-        cw_raw = load.tile([P, 4, C], BF16, name="cw_raw", tag="g_raw")
+        wsm = const.tile([P, 5, NCT, 64], BF16, name="wsm")
+        for m in range(5):
+            nc.scalar.dma_start(
+                out=wsm[:, m, :, 0 : KT * KT], in_=w[TAPS[m]].rearrange("(ct c) r s -> c ct (r s)", c=P)
+            )
+
+        blk = {}
+
+        def load_group(gi):
+            b, k = divmod(gi, NT // 4)
+            xs = load.tile([P, NCT, XE], BF16, name="xs")
+            lo = GRP * k - XPAD
+            clo, chi = max(lo, 0), min(lo + XE, HW)
+            if clo > lo:
+                nc.gpsimd.memset(xs[:, :, 0 : clo - lo], 0.0)
+            if chi < lo + XE:
+                nc.gpsimd.memset(xs[:, :, chi - lo : XE], 0.0)
+            nc.sync.dma_start(out=xs[:, :, clo - lo : chi - lo], in_=x_v[b][:, :, clo:chi])
+            g_raw = load.tile([P, 4, GRP], BF16, name="g_raw")
+            nc.sync.dma_start(out=g_raw[:], in_=g_v[b][:, :, GRP * k : GRP * k + GRP])
+            blk[gi] = {"xs": xs, "g_raw": g_raw}
+
+        load_group(0)
+
+        wrow = const.tile([P, 5, NCT, WW], BF16, name="wrow")
+        for m in range(5):
+            for ct in range(NCT):
+                rows = wrow[:, m, ct, 0:PER].rearrange("c (r j) -> c r j", j=W)
+                src = wsm[:, m, ct, 0 : KT * KT].rearrange("c (r s) -> c r s", s=KT)
+                nc.vector.tensor_copy(
+                    out=rows[:, :, 0:70].rearrange("c r (jb s) -> c r jb s", s=KT),
+                    in_=src.unsqueeze(2).to_broadcast([P, KT, 10, KT]),
+                )
+                nc.vector.tensor_copy(out=rows[:, :, 70:72], in_=src[:, :, 0:2])
+        nc.vector.memset(wrow[:, 3, :, 0:PER:W], 0.0)
+        nc.vector.memset(wrow[:, 4, :, W - 1 : PER : W], 0.0)
+        nc.vector.tensor_copy(out=wrow[:, :, :, PER:WW], in_=wrow[:, :, :, 0:P])
+
+        cw_raw = const.tile([P, 4, C], BF16, name="cw_raw")
         nc.sync.dma_start(out=cw_raw[:], in_=conv_w.rearrange("(p j) c -> p j c", j=4))
-        cw_grp = quant.tile([P, C, 4], BF16, name="cw_grp", tag="g_grp", align_bytes=64)
+        cw_grp = const.tile([P, C, 4], BF16, name="cw_grp", align_bytes=64)
         nc.vector.tensor_copy(out=cw_grp[:], in_=cw_raw[:].rearrange("p j c -> p c j"))
         cw_q = const.tile([P, C], U32, name="cw_q", align_bytes=64)
         cw_s = const.tile([P, C], U8, name="cw_s", align_bytes=64)
@@ -96,177 +99,102 @@ def tile_lablock_t_kernel(tc, x, w, conv_w, conv_b, grad_out, out):
             out=cw_q[:].bitcast(E4X4), scales=cw_s[:], in_=cw_grp[:].rearrange("p c j -> p (c j)")
         )
 
-        wsm = const.tile([P, 5, NCT, 64], BF16, name="wsm")
-        for n in range(5):
-            nc.scalar.dma_start(out=wsm[:, n, :, 0 : KT * KT], in_=w[n].rearrange("(ct c) r s -> c ct (r s)", c=P))
-        wrow = const.tile([P, 5, NCT, BW], BF16, name="wrow")
-        for n in range(5):
-            for ct in range(NCT):
-                rows = wrow[:, n, ct, MG : MG + BLK].rearrange("c (r j) -> c r j", j=W)
-                src = wsm[:, n, ct, 0 : KT * KT].rearrange("c (r s) -> c r s", s=KT)
-                copy = nc.scalar.copy if n in (2, 3) else nc.vector.tensor_copy
-                copy(
-                    out=rows[:, :, 0:70].rearrange("c r (jb s) -> c r jb s", s=KT),
-                    in_=src.unsqueeze(2).to_broadcast([P, KT, 10, KT]),
-                )
-                copy(out=rows[:, :, 70:72], in_=src[:, :, 0:2])
-        nc.vector.tensor_copy(out=wrow[:, :, :, 0:MG], in_=wrow[:, :, :, BLK : BLK + MG])
-        nc.vector.tensor_copy(out=wrow[:, :, :, BLK + MG : BW], in_=wrow[:, :, :, MG : 2 * MG])
-        nc.vector.memset(wrow[:, 3, :, MG:BW:W], 0.0)
-        nc.vector.memset(wrow[:, 4, :, MG - 1 : BW : W], 0.0)
+        ring = const.tile([P, 5 * NCT * RING + RING], F32, name="ring")
+        ring_v = ring[:, 0 : 5 * NCT * RING].rearrange("c (m ct r) -> c m ct r", ct=NCT, r=RING)
 
-        cleared = {(0, 3): (1, P), (3, 4): (0, P - 1), (0, 2): (MG, P), (3, 1): (0, P - MG)}
-        wt = const.tile([P, 4, 5, C], BF16, name="wt")
+        def ring_cols(m, lo, hi):
+            return ring_v[:, m, :, lo:hi]
 
-        def turn_weights(a):
-            for n in range(1, 5):
-                wps = psum.tile([P, C], BF16, name="wps", tag="ob%d" % (n % NCT))
-                for ct in range(NCT):
-                    nc.tensor.transpose(
-                        out=wps[:, ct * P : (ct + 1) * P],
-                        in_=wrow[:, n, ct, P * a : P * a + P],
-                        identity=ident_b[:],
-                    )
-                if (a, n) in cleared:
-                    nc.scalar.activation(
-                        out=wt[:, a, n, :], in_=wps[:], func=ACT.Copy, scale=keep[cleared[(a, n)]][:]
-                    )
-                elif n % 2 == 0:
-                    nc.scalar.copy(out=wt[:, a, n, :], in_=wps[:])
-                else:
-                    nc.vector.tensor_copy(out=wt[:, a, n, :], in_=wps[:])
+        nc.vector.memset(ring_cols(2, 0, W), 0.0)
+        nc.vector.memset(ring_cols(4, 0, 1), 0.0)
 
-        steps = []
-        for b in range(NB):
-            for k in range(NBLK):
-                ncol = min(BLK, HW - BLK * k)
-                ntile = (MG + ncol + P - 1) // P
-                for a in range(ntile):
-                    steps.append((b, k, a, ntile, back_moves(k, a, ntile)))
-        first = {}
-        last = {}
-        for si, (b, k, a, ntile, moves) in enumerate(steps):
-            for mi, mv in enumerate(moves):
-                if (b, mv[0]) not in first:
-                    first[(b, mv[0])] = (si, mi)
-                last[(b, mv[0])] = (si, mi)
-
-        banks = {}
-        blk = {}
+        nstep = NB * NT
         st = {}
-        nstep = len(steps)
-        blocks = [(b, k, ntile) for (b, k, a, ntile, moves) in steps if a == 0]
-        block_of = []
-        for si, (b, k, a, ntile, moves) in enumerate(steps):
-            block_of.append(len([1 for s2 in steps[: si + 1] if s2[2] == 0]) - 1)
 
-        def load_block(bi):
-            b, k, ntile = blocks[bi]
-            base = BLK * k - MG
-            xs = load.tile([P, NCT, XE], BF16, name="xs")
-            lo = base - XPAD
-            hi = lo + XE
-            clo, chi = max(lo, 0), min(hi, HW)
-            if clo != lo or chi != hi:
-                nc.gpsimd.memset(xs[:], 0.0)
-            nc.sync.dma_start(out=xs[:, :, clo - lo : chi - lo], in_=x_v[b][:, :, clo:chi])
-            g_raw = load.tile([P, 4, BW], BF16, name="g_raw")
-            lo = base
-            hi = lo + BW
-            clo, chi = max(lo, 0), min(hi, HW)
-            if clo != lo or chi != hi:
-                nc.gpsimd.memset(g_raw[:], 0.0)
-            nc.sync.dma_start(out=g_raw[:, :, clo - lo : chi - lo], in_=g_v[b][:, :, clo:chi])
-            blk[bi] = {"xs": xs, "g_raw": g_raw}
+        def tile_of(si):
+            b, a = divmod(si, NT)
+            return blk[si // 4], P * (si % 4), (P * a) % PER
 
-        def regroup_block(bi):
-            gw = blocks[bi][2] * P
-            g_grp = quant.tile([P, BW, 4], BF16, name="g_grp", align_bytes=64)
-            nc.scalar.copy(
-                out=g_grp[:, 0:gw, :], in_=blk[bi]["g_raw"][:, :, 0:gw].rearrange("p j q -> p q j")
-            )
-            blk[bi]["g_grp"] = g_grp
+        def regroup(si):
+            bl, col, e0 = tile_of(si)
+            g_grp = quant.tile([P, P, 4], BF16, name="g_grp", align_bytes=64)
+            nc.scalar.copy(out=g_grp[:], in_=bl["g_raw"][:, :, col : col + P].rearrange("p j q -> p q j"))
+            st[si]["g_grp"] = g_grp
 
-        def quantise_block(bi):
-            gw = blocks[bi][2] * P
-            g_q = quant.tile([P, BW], U32, name="g_q", align_bytes=64)
-            g_s = quant.tile([P, BW], U8, name="g_s", align_bytes=64)
+        def quantise(si):
+            g_q = quant.tile([P, P], U32, name="g_q", align_bytes=64)
+            g_s = quant.tile([P, P], U8, name="g_s", align_bytes=64)
             nc.vector.quantize_mx(
-                out=g_q[:, 0:gw].bitcast(E5X4),
-                scales=g_s[:, 0:gw],
-                in_=blk[bi]["g_grp"][:, 0:gw, :].rearrange("p q j -> p (q j)"),
+                out=g_q[:].bitcast(E5X4), scales=g_s[:], in_=st[si]["g_grp"][:].rearrange("p q j -> p (q j)")
             )
-            blk[bi]["g_q"] = g_q
-            blk[bi]["g_s"] = g_s
+            st[si]["g_q"] = g_q
+            st[si]["g_s"] = g_s
 
-        def product(si, n, eng, c0=0, c1=NCT):
-            a = steps[si][2]
-            if si not in st:
-                st[si] = {"prod": work.tile([P, 5, NCT, P], F32, name="prod", bufs=4)}
-            e0 = P * a + XPAD + OFF[n]
-            eng.tensor_tensor(
-                out=st[si]["prod"][:, n, c0:c1, :],
-                in0=blk[block_of[si]]["xs"][:, c0:c1, e0 : e0 + P],
-                in1=wrow[:, n, c0:c1, P * a : P * a + P],
-                op=ALU.mult,
-            )
+        def products(si, taps, eng):
+            bl, col, e0 = tile_of(si)
+            for m in taps:
+                x0 = XPAD + col + OFF[m]
+                eng.tensor_tensor(
+                    out=st[si]["prod"][:, m, :, :],
+                    in0=bl["xs"][:, :, x0 : x0 + P],
+                    in1=wrow[:, m, :, e0 : e0 + P],
+                    op=ALU.mult,
+                )
 
-        def turn_products(si, taps, opens, closes):
-            if opens:
-                st[si]["at_ps"] = psum.tile([P, C], F32, name="at_ps", tag="at_ps", bufs=2)
-            for ti, n in enumerate(taps):
+        def turn(out, pieces):
+            for pi, piece in enumerate(pieces):
                 for ct in range(NCT):
                     nc.tensor.matmul(
-                        out=st[si]["at_ps"][:, ct * P : (ct + 1) * P],
-                        lhsT=st[si]["prod"][:, n, ct, :],
+                        out=out[:, ct * P : (ct + 1) * P],
+                        lhsT=piece(ct),
                         rhs=ident_f[:],
                         is_transpose=True,
-                        start=(opens and ti == 0 and ct == 0),
-                        stop=(closes and ti == len(taps) - 1 and ct == NCT - 1),
+                        start=(pi == 0 and ct == 0),
+                        stop=(pi == len(pieces) - 1 and ct == NCT - 1),
                     )
 
-        def turn_x_and_multiply(si, wi):
-            xt_ps = psum.tile([P, 2 * C], BF16, name="xt_ps")
-            if wi is not None:
-                aw = steps[wi][2]
-                for ct in range(NCT):
-                    nc.tensor.transpose(
-                        out=xt_ps[:, C + ct * P : C + (ct + 1) * P],
-                        in_=wrow[:, 0, ct, P * aw : P * aw + P],
-                        identity=ident_b[:],
-                    )
-                st[wi]["w0_ps"] = xt_ps
-            if si is None:
-                return
-            a = steps[si][2]
-            bl = blk[block_of[si]]
-            e0 = P * a + XPAD
+        def turn_products(si):
+            prod = st[si]["prod"]
+            at_ps = psum.tile([P, C], F32, name="at_ps", bufs=2)
+            turn(at_ps, [lambda ct, m=m: prod[:, m, ct, :] for m in V_TAPS + G_TAPS])
+            st[si]["at_ps"] = at_ps
+
+        def turn_x_and_multiply(si):
+            bl, col, e0 = tile_of(si)
+            xt_ps = psum.tile([P, C], BF16, name="xt_ps")
             for ct in range(NCT):
                 nc.tensor.transpose(
-                    out=xt_ps[:, ct * P : (ct + 1) * P], in_=bl["xs"][:, ct, e0 : e0 + P], identity=ident_b[:]
+                    out=xt_ps[:, ct * P : (ct + 1) * P],
+                    in_=bl["xs"][:, ct, XPAD + col : XPAD + col + P],
+                    identity=ident_b[:],
                 )
             g1_ps = psum.tile([P, C], F32, name="g1_ps")
             nc.tensor.matmul_mx(
                 out=g1_ps[:],
-                lhsT=bl["g_q"][:, a * P : (a + 1) * P].bitcast(E5X4),
-                lhsT_scale=bl["g_s"][:, a * P : (a + 1) * P],
+                lhsT=st[si]["g_q"][:].bitcast(E5X4),
+                lhsT_scale=st[si]["g_s"][:],
                 rhs=cw_q[:].bitcast(E4X4),
                 rhs_scale=cw_s[:],
                 start=True,
                 stop=True,
             )
-            g1 = work.tile([P, C], F32, name="g1")
-            nc.scalar.copy(out=g1[:], in_=g1_ps[:])
             st[si]["xt_ps"] = xt_ps
             st[si]["g1_ps"] = g1_ps
+
+        def copy_g1(si):
+            g1 = work.tile([P, C], F32, name="g1", bufs=7)
+            nc.scalar.copy(out=g1[:], in_=st[si]["g1_ps"][:])
             st[si]["g1"] = g1
 
-        def maximum_and_exp(si):
-            s_ = st[si]
+        def maximum(si):
             mx = small.tile([P, 1], F32, name="mx")
-            nc.vector.tensor_reduce(out=mx[:], in_=s_["at_ps"][:], axis=AX.X, op=ALU.max)
+            nc.vector.tensor_reduce(out=mx[:], in_=st[si]["at_ps"][:], axis=AX.X, op=ALU.max)
+            st[si]["mx"] = mx
+
+        def exponential(si):
+            s_ = st[si]
             nmx = small.tile([P, 1], F32, name="nmx")
-            nc.scalar.mul(out=nmx[:], in_=mx[:], mul=-1.0)
+            nc.scalar.mul(out=nmx[:], in_=s_["mx"][:], mul=-1.0)
             ex = work.tile([P, C], F32, name="ex")
             ssum = small.tile([P, 1], F32, name="ssum")
             nc.scalar.activation(
@@ -276,26 +204,24 @@ def tile_lablock_t_kernel(tc, x, w, conv_w, conv_b, grad_out, out):
             s_["ssum"] = ssum
 
         def one_over_sum(si):
-            s_ = st[si]
             rs = small.tile([P, 1], F32, name="rs")
-            nc.vector.reciprocal(out=rs[:], in_=s_["ssum"][:])
-            s_["rs"] = rs
+            nc.vector.reciprocal(out=rs[:], in_=st[si]["ssum"][:])
+            st[si]["rs"] = rs
 
         def att_times_g1(si):
             s_ = st[si]
-            rs = s_["rs"]
-            ag = work.tile([P, C], F32, name="ag")
+            ag = work.tile([P, C], F32, name="ag", bufs=6)
             nc.vector.scalar_tensor_tensor(
-                out=ag[:], in0=s_["ex"][:], scalar=rs[:], in1=s_["g1_ps"][:], op0=ALU.mult, op1=ALU.mult
+                out=ag[:], in0=s_["ex"][:], scalar=s_["rs"][:], in1=s_["g1_ps"][:], op0=ALU.mult, op1=ALU.mult
             )
             s_["ag"] = ag
 
         def att_times_t(si):
             s_ = st[si]
-            att_t = work.tile([P, C], F32, name="att_t", bufs=2)
+            att_t = work.tile([P, C], F32, name="att_t")
             rr = small.tile([P, 1], F32, name="rr")
             nc.vector.scalar_tensor_tensor(
-                out=att_t[:], in0=s_["ag"][:], scalar=1.0, in1=s_["xt_ps"][:, 0:C], op0=ALU.mult, op1=ALU.mult,
+                out=att_t[:], in0=s_["ag"][:], scalar=1.0, in1=s_["xt_ps"][:], op0=ALU.mult, op1=ALU.mult,
                 accum_out=rr[:],
             )
             s_["att_t"] = att_t
@@ -309,140 +235,152 @@ def tile_lablock_t_kernel(tc, x, w, conv_w, conv_b, grad_out, out):
             )
             s_["nrr"] = nrr
 
-        def logit_gradient(si):
+        def minus_att_times_r(si):
             s_ = st[si]
-            da = work.tile([P, C], F32, name="da", bufs=2)
-            nc.vector.scalar_tensor_tensor(
-                out=da[:], in0=s_["ex"][:], scalar=s_["nrr"][:], in1=s_["att_t"][:], op0=ALU.mult, op1=ALU.add
-            )
-            s_["da"] = da
+            ar = work.tile([P, C], F32, name="ar")
+            nc.scalar.activation(out=ar[:], in_=s_["ex"][:], func=ACT.Copy, scale=s_["nrr"][:])
+            s_["ar"] = ar
 
-        def weighted_gradient(si):
-            b, k, a, ntile, moves = steps[si]
+        def turn_logit_gradient(si):
             s_ = st[si]
-            m = work.tile([P, 5, C], F32, name="m")
-            nc.vector.tensor_tensor(
-                out=m[:, 1:5, :],
-                in0=s_["da"][:].unsqueeze(1).to_broadcast([P, 4, C]),
-                in1=wt[:, a, 1:5, :],
-                op=ALU.mult,
+            da_ps = psum.tile([P, C], F32, name="da_ps", bufs=2)
+            turn(da_ps, [lambda ct, t=t: s_[t][:, ct * P : (ct + 1) * P] for t in ("att_t", "ar")])
+            s_["da_ps"] = da_ps
+
+        def weigh(si, m0, m1, q0, q1):
+            bl, col, e0 = tile_of(si)
+            nm = m1 - m0
+            da = st[si]["da_ps"][:].rearrange("c (ct q) -> c ct q", q=P)[:, :, q0:q1]
+            first = (P * si + OFF[m0] + q0) % RING
+            if nm == 1:
+                nc.vector.tensor_tensor(
+                    out=ring_cols(m0, first, first + q1 - q0),
+                    in0=da,
+                    in1=wrow[:, m0, :, e0 + q0 : e0 + q1],
+                    op=ALU.mult,
+                )
+            else:
+                step = NCT * RING + OFF[m0 + 1] - OFF[m0]
+                base = m0 * NCT * RING + first
+                target = ring[:, base : base + nm * step]
+                target = target.rearrange("c (m s) -> c m s", s=step)[:, :, 0 : NCT * RING]
+                target = target.rearrange("c m (ct r) -> c m ct r", r=RING)[:, :, :, 0:P]
+                nc.vector.tensor_tensor(
+                    out=target,
+                    in0=da.unsqueeze(1).to_broadcast([P, nm, NCT, P]),
+                    in1=wrow[:, m0:m1, :, e0 : e0 + P],
+                    op=ALU.mult,
+                )
+
+        def weigh_plan(si):
+            if si % 4 == 0:
+                part_a = [(3, 4, 1, P), (4, 5, 0, P)]
+                part_b = [(1, 3, 0, P), (0, 1, W, P)]
+                if si > 0:
+                    part_a.append((3, 4, 0, 1))
+                if si % NT != 0:
+                    part_b.append((0, 1, 0, W))
+            elif si % 4 == 3:
+                part_a = [(3, 4, 0, P), (4, 5, 0, P - 1)]
+                part_b = [(0, 2, 0, P), (2, 3, 0, P - W)]
+                if si < nstep - 1:
+                    part_a.append((4, 5, P - 1, P))
+                if si % NT != NT - 1:
+                    part_b.append((2, 3, P - W, P))
+            else:
+                part_a = [(3, 5, 0, P)]
+                part_b = [(0, 3, 0, P)]
+            return part_a, part_b
+
+        def weigh_part(si, part):
+            if si < nstep:
+                for m0, m1, q0, q1 in weigh_plan(si)[part]:
+                    weigh(si, m0, m1, q0, q1)
+            if part == 1:
+                if si % NT == 0 and si > 0:
+                    nc.vector.memset(ring_cols(0, RING - W, RING), 0.0)
+                if si % NT == NT - 1 and si < nstep - 1:
+                    nc.vector.memset(ring_cols(2, 0, W), 0.0)
+                if si == nstep:
+                    nc.vector.memset(ring_cols(3, RING - 1, RING), 0.0)
+
+        def turn_sum(si):
+            q = P * si % RING
+            sum_ps = psum.tile([P, C], F32, name="sum_ps")
+            turn(sum_ps, [lambda ct, m=m: ring_cols(m, q, q + P)[:, ct, :] for m in range(5)])
+            st[si]["sum_ps"] = sum_ps
+
+        def copy_sum(si):
+            total = work.tile([P, C], F32, name="total")
+            nc.scalar.copy(out=total[:], in_=st[si]["sum_ps"][:])
+            st[si]["total"] = total
+
+        def turn_out(si):
+            s_ = st[si]
+            out_ps = psum.tile([P, C], F32, name="out_ps")
+            turn(out_ps, [lambda ct, t=t: s_[t][:, ct * P : (ct + 1) * P] for t in ("g1", "ag", "total")])
+            s_["out_ps"] = out_ps
+
+        def copy_out(si):
+            b, a = divmod(si, NT)
+            if si % 4 == 0:
+                osb = store.tile([P, NCT, GRP], F32, name="osb")
+                st["osb"] = osb
+            q = P * (si % 4)
+            osb = st["osb"]
+            nc.scalar.copy(
+                out=osb[:, :, q : q + P], in_=st[si]["out_ps"][:].rearrange("c (ct q) -> c ct q", q=P)
             )
-            nc.vector.tensor_tensor(out=m[:, 0, :], in0=s_["da"][:], in1=s_["w0_ps"][:, C : 2 * C], op=ALU.mult)
-            terms = {}
-            s_["terms"] = terms
-            if si > 0:
-                old = st[si - 1]["terms"]
-                terms["prev_m4"] = old["m4"]
-                terms["prev_m2"] = old["m2"]
-                if "down_next_bank" in old:
-                    terms["down_next_bank"] = old["down_next_bank"]
-            terms["g1"] = s_["g1"][:]
-            terms["ag"] = s_["ag"][:]
-            for n in range(5):
-                terms["m%d" % n] = m[:, n, :]
+            if si >= nstep - 4:
+                nc.sync.dma_start(out=o_v[b][:, :, P * a : P * a + P], in_=osb[:, :, q : q + P])
+            elif si % 4 == 3:
+                nc.sync.dma_start(out=o_v[b][:, :, P * (a - 3) : P * (a + 1)], in_=osb[:])
 
-        def edge_pieces(si, names):
-            b, k, a, ntile, moves = steps[si]
-            terms = st[si]["terms"]
-            for name, n, rows, wanted in (
-                ("up_prev_bank", 1, (MG, MG + W), a == 0 and k > 0),
-                ("up_first", 1, (W, P), a == 0 and ntile > 1),
-                ("down_last", 2, (0, P - W), a == 3),
-                ("down_next_bank", 2, (52, 52 + W), a == 3),
-            ):
-                if wanted and name in names:
-                    piece = edge.tile([P, C], F32, name=name)
-                    nc.scalar.activation(out=piece[:], in_=terms["m%d" % n], func=ACT.Copy, scale=keep[rows][:])
-                    terms[name] = piece[:]
-
-        def back(si, lo, hi):
-            b, k, a, ntile, moves = steps[si]
-            terms = st[si]["terms"]
-            for mi, (bank, term, s, col) in enumerate(moves):
-                if mi < lo or mi >= hi:
-                    continue
-                if first[(b, bank)] == (si, mi):
-                    banks[bank] = [
-                        psum.tile([P, C], F32, name="ob%d" % ct, tag="ob%d" % ct) for ct in range(NCT)
-                    ]
-                for ct in range(NCT):
-                    nc.tensor.matmul(
-                        out=banks[bank][ct][:, col : col + P],
-                        lhsT=terms[term][:, ct * P : (ct + 1) * P],
-                        rhs=rot[s][:],
-                        is_transpose=True,
-                        start=(first[(b, bank)] == (si, mi)),
-                        stop=(last[(b, bank)] == (si, mi)),
-                    )
-                if last[(b, bank)] == (si, mi):
-                    ncol = min(BLK, HW - BLK * bank)
-                    osb = store.tile([P, NCT, BLK], F32, name="osb")
-                    for ct in range(NCT):
-                        nc.scalar.copy(out=osb[:, ct, 0:ncol], in_=banks[bank][ct][:, MG : MG + ncol])
-                    nc.sync.dma_start(
-                        out=o_v[b][:, :, BLK * bank : BLK * bank + ncol], in_=osb[:, :, 0:ncol]
-                    )
-
-        def block_starting_at(si):
-            return block_of[si] if 0 <= si < nstep and steps[si][2] == 0 else None
-
-        load_block(0)
-        regroup_block(0)
-        quantise_block(0)
         ctx.enter_context(tc.manual_schedule())
-        for i in range(-3, nstep + 1):
-            tb, t0, t1, t2, t3 = i - 1, i, i + 1, i + 2, i + 3
-            vb = 0 <= tb
+        for i in range(-3, nstep + 4):
+            t0, t1, t2, t3 = i, i + 1, i + 2, i + 3
+            te, td, to = i - 1, i - 3, i - 4
             v0 = 0 <= t0 < nstep
             v1 = 0 <= t1 < nstep
             v2 = 0 <= t2 < nstep
             v3 = t3 < nstep
-            closing = 1 if (v0 and steps[t0][2] == 0 and steps[t0][1] > 0) else 0
-            closed_b = 1 if (vb and steps[tb][2] == 0 and steps[tb][1] > 0) else 0
-            if block_starting_at(i + LEAD_LOAD) is not None:
-                load_block(block_starting_at(i + LEAD_LOAD))
-            if block_starting_at(i + LEAD_REGROUP) is not None:
-                regroup_block(block_starting_at(i + LEAD_REGROUP))
+            if (i + 7) % 4 == 0 and 1 <= (i + 7) // 4 < nstep // 4:
+                load_group((i + 7) // 4)
             if v3:
-                product(t3, 4, nc.gpsimd)
-                product(t3, 3, nc.gpsimd)
+                st[t3] = {"prod": work.tile([P, 5, NCT, P], F32, name="prod", bufs=2)}
             if v0:
                 att_times_g1(t0)
             if v1:
-                maximum_and_exp(t1)
+                maximum(t1)
+                exponential(t1)
             if v0:
                 att_times_t(t0)
-            if v3:
-                product(t3, 0, nc.vector)
-            if v2:
-                turn_products(t2, (4, 0), True, False)
+            if 0 <= td < nstep:
+                turn_sum(td)
+            if 0 <= te <= nstep:
+                weigh_part(te, 0)
             if v0:
                 minus_r_over_sum(t0)
-            if v3:
-                product(t3, 1, nc.vector)
-            if v2:
-                turn_products(t2, (1,), False, False)
-            if vb:
-                back(tb, closed_b, 5)
-            if block_starting_at(i + LEAD_QUANT) is not None:
-                quantise_block(block_starting_at(i + LEAD_QUANT))
+                minus_att_times_r(t0)
+            if 0 <= td < nstep:
+                copy_sum(td)
+            if 0 <= to < nstep:
+                turn_out(to)
+                copy_out(to)
+            if 0 <= te <= nstep:
+                weigh_part(te, 1)
+            if v1:
+                turn_x_and_multiply(t1)
+                copy_g1(t1)
             if v0:
-                logit_gradient(t0)
-            if v0 or v1:
-                turn_x_and_multiply(t1 if v1 else None, t0 if v0 else None)
-            if v3:
-                product(t3, 2, nc.vector)
-            if v2:
-                turn_products(t2, (2, 3), False, True)
-            if vb:
-                back(tb, 5, 99)
-            if -2 <= i < 0:
-                turn_weights(2 * (i + 2))
-                turn_weights(2 * (i + 2) + 1)
+                turn_logit_gradient(t0)
             if v1:
                 one_over_sum(t1)
-            if v0:
-                weighted_gradient(t0)
-                edge_pieces(t0, ("up_prev_bank",))
-                back(t0, 0, closing)
-                edge_pieces(t0, ("up_first", "down_last", "down_next_bank"))
+            if v2:
+                quantise(t2)
+            if v3:
+                regroup(t3)
+                products(t3, G_TAPS, nc.gpsimd)
+                products(t3, V_TAPS, nc.vector)
+            if v2:
+                turn_products(t2)

@@ -348,6 +348,8 @@ def tile_lablock_t_kernel(tc, x, w, conv_w, conv_b, grad_out, out):
                 load_group((i + 7) // 4)
             if v3:
                 st[t3] = {"prod": work.tile([P, 5, NCT, P], F32, name="prod", bufs=2)}
+            if 0 <= te < nstep:
+                turn_logit_gradient(te)
             if v0:
                 att_times_g1(t0)
             if v1:
@@ -372,8 +374,6 @@ def tile_lablock_t_kernel(tc, x, w, conv_w, conv_b, grad_out, out):
             if v1:
                 turn_x_and_multiply(t1)
                 copy_g1(t1)
-            if v0:
-                turn_logit_gradient(t0)
             if v1:
                 one_over_sum(t1)
             if v2:

@@ -115,20 +115,22 @@ def tile_lablock_t_kernel(tc, x, w, conv_w, conv_b, grad_out, out):
             b, a = divmod(si, NT)
             return blk[si // 4], P * (si % 4), (P * a) % PER
 
-        def regroup(si):
-            bl, col, e0 = tile_of(si)
-            g_grp = quant.tile([P, P, 4], BF16, name="g_grp", align_bytes=64)
-            nc.scalar.copy(out=g_grp[:], in_=bl["g_raw"][:, :, col : col + P].rearrange("p j q -> p q j"))
-            st[si]["g_grp"] = g_grp
+        pairs = {}
 
-        def quantise(si):
-            g_q = quant.tile([P, P], U32, name="g_q", align_bytes=64)
-            g_s = quant.tile([P, P], U8, name="g_s", align_bytes=64)
+        def regroup_pair(si):
+            bl, col, e0 = tile_of(si)
+            g_grp = quant.tile([P, 2 * P, 4], BF16, name="g_grp", align_bytes=64)
+            nc.scalar.copy(out=g_grp[:], in_=bl["g_raw"][:, :, col : col + 2 * P].rearrange("p j q -> p q j"))
+            pairs[si] = {"g_grp": g_grp}
+
+        def quantise_pair(si):
+            g_q = quant.tile([P, 2 * P], U32, name="g_q", align_bytes=64)
+            g_s = quant.tile([P, 2 * P], U8, name="g_s", align_bytes=64)
             nc.vector.quantize_mx(
-                out=g_q[:].bitcast(E5X4), scales=g_s[:], in_=st[si]["g_grp"][:].rearrange("p q j -> p (q j)")
+                out=g_q[:].bitcast(E5X4), scales=g_s[:], in_=pairs[si]["g_grp"][:].rearrange("p q j -> p (q j)")
             )
-            st[si]["g_q"] = g_q
-            st[si]["g_s"] = g_s
+            pairs[si]["g_q"] = g_q
+            pairs[si]["g_s"] = g_s
 
         def products(si, taps, eng):
             bl, col, e0 = tile_of(si)
@@ -155,31 +157,33 @@ def tile_lablock_t_kernel(tc, x, w, conv_w, conv_b, grad_out, out):
 
         def turn_products(si):
             prod = st[si]["prod"]
-            at_ps = psum.tile([P, C], F32, name="at_ps", bufs=2)
+            at_ps = psum.tile([P, C], F32, name="at_ps")
             turn(at_ps, [lambda ct, m=m: prod[:, m, ct, :] for m in V_TAPS + G_TAPS])
             st[si]["at_ps"] = at_ps
 
-        def turn_x_and_multiply(si):
-            bl, col, e0 = tile_of(si)
-            xt_ps = psum.tile([P, C], BF16, name="xt_ps")
-            for ct in range(NCT):
-                nc.tensor.transpose(
-                    out=xt_ps[:, ct * P : (ct + 1) * P],
-                    in_=bl["xs"][:, ct, XPAD + col : XPAD + col + P],
-                    identity=ident_b[:],
+        def turn_x_and_multiply_pair(si):
+            xt_ps = psum.tile([P, 2, C], BF16, name="xt_ps")
+            for u in range(2):
+                bl, col, e0 = tile_of(si + u)
+                for ct in range(NCT):
+                    nc.tensor.transpose(
+                        out=xt_ps[:, u, ct * P : (ct + 1) * P],
+                        in_=bl["xs"][:, ct, XPAD + col : XPAD + col + P],
+                        identity=ident_b[:],
+                    )
+                st[si + u]["xt_ps"] = xt_ps[:, u, :]
+            for u in range(2):
+                g1_ps = psum.tile([P, C], F32, name="g1_ps", bufs=2)
+                nc.tensor.matmul_mx(
+                    out=g1_ps[:],
+                    lhsT=pairs[si]["g_q"][:, u * P : (u + 1) * P].bitcast(E5X4),
+                    lhsT_scale=pairs[si]["g_s"][:, u * P : (u + 1) * P],
+                    rhs=cw_q[:].bitcast(E4X4),
+                    rhs_scale=cw_s[:],
+                    start=True,
+                    stop=True,
                 )
-            g1_ps = psum.tile([P, C], F32, name="g1_ps")
-            nc.tensor.matmul_mx(
-                out=g1_ps[:],
-                lhsT=st[si]["g_q"][:].bitcast(E5X4),
-                lhsT_scale=st[si]["g_s"][:],
-                rhs=cw_q[:].bitcast(E4X4),
-                rhs_scale=cw_s[:],
-                start=True,
-                stop=True,
-            )
-            st[si]["xt_ps"] = xt_ps
-            st[si]["g1_ps"] = g1_ps
+                st[si + u]["g1_ps"] = g1_ps
 
         def copy_g1(si):
             g1 = work.tile([P, C], F32, name="g1", bufs=7)
@@ -221,7 +225,7 @@ def tile_lablock_t_kernel(tc, x, w, conv_w, conv_b, grad_out, out):
             att_t = work.tile([P, C], F32, name="att_t")
             rr = small.tile([P, 1], F32, name="rr")
             nc.vector.scalar_tensor_tensor(
-                out=att_t[:], in0=s_["ag"][:], scalar=1.0, in1=s_["xt_ps"][:], op0=ALU.mult, op1=ALU.mult,
+                out=att_t[:], in0=s_["ag"][:], scalar=1.0, in1=s_["xt_ps"], op0=ALU.mult, op1=ALU.mult,
                 accum_out=rr[:],
             )
             s_["att_t"] = att_t
@@ -371,15 +375,17 @@ def tile_lablock_t_kernel(tc, x, w, conv_w, conv_b, grad_out, out):
                 copy_out(to)
             if 0 <= te <= nstep:
                 weigh_part(te, 1)
-            if v1:
-                turn_x_and_multiply(t1)
+            if v1 and t1 % 2 == 0:
+                turn_x_and_multiply_pair(t1)
                 copy_g1(t1)
+                copy_g1(t1 + 1)
             if v1:
                 one_over_sum(t1)
-            if v2:
-                quantise(t2)
+            if v2 and t2 % 2 == 0:
+                quantise_pair(t2)
+            if v3 and t3 % 2 == 0:
+                regroup_pair(t3)
             if v3:
-                regroup(t3)
                 products(t3, G_TAPS, nc.gpsimd)
                 products(t3, V_TAPS, nc.vector)
             if v2:

@@ -21,13 +21,17 @@ NT = HW // P
 GRP = 4 * P
 PER = KT * W
 WW = PER + P
-TAPS = (1, 0, 2, 3, 4)
-OFF = (-W, 0, W, -1, 1)
+TAPS = (1, 2, 0, 3, 4)
+OFF = (-W, W, 0, -1, 1)
 XPAD = 80
 XE = GRP + 2 * XPAD
 RING = 4 * P
-G_TAPS = (2, 3, 4)
-V_TAPS = (0, 1)
+PAD = 4
+RS = RING + 2 * PAD
+SHIFT = (0, 0, 0, -1, 1)
+NV = 2
+G_TAPS = (0, 1, 2)
+V_TAPS = (3, 4)
 FLOPS = 2 * O * C * NB * HW
 
 
@@ -80,33 +84,39 @@ def tile_lablock_t_kernel(tc, x, w, conv_w, conv_b, grad_out, out):
             for ct in range(NCT):
                 rows = wrow[:, m, ct, 0:PER].rearrange("c (r j) -> c r j", j=W)
                 src = wsm[:, m, ct, 0 : KT * KT].rearrange("c (r s) -> c r s", s=KT)
-                nc.vector.tensor_copy(
+                nc.vector.tensor_scalar(
                     out=rows[:, :, 0:70].rearrange("c r (jb s) -> c r jb s", s=KT),
-                    in_=src.unsqueeze(2).to_broadcast([P, KT, 10, KT]),
+                    in0=src.unsqueeze(2).to_broadcast([P, KT, 10, KT]),
+                    scalar1=-1.0,
+                    scalar2=None,
+                    op0=ALU.mult,
                 )
-                nc.vector.tensor_copy(out=rows[:, :, 70:72], in_=src[:, :, 0:2])
+                nc.vector.tensor_scalar(
+                    out=rows[:, :, 70:72], in0=src[:, :, 0:2], scalar1=-1.0, scalar2=None, op0=ALU.mult
+                )
         nc.vector.memset(wrow[:, 3, :, 0:PER:W], 0.0)
         nc.vector.memset(wrow[:, 4, :, W - 1 : PER : W], 0.0)
-        nc.vector.tensor_copy(out=wrow[:, :, :, PER:WW], in_=wrow[:, :, :, 0:P])
 
         cw_raw = const.tile([P, 4, C], BF16, name="cw_raw")
         nc.sync.dma_start(out=cw_raw[:], in_=conv_w.rearrange("(p j) c -> p j c", j=4))
         cw_grp = const.tile([P, C, 4], BF16, name="cw_grp", align_bytes=64)
-        nc.vector.tensor_copy(out=cw_grp[:], in_=cw_raw[:].rearrange("p j c -> p c j"))
+        nc.scalar.copy(out=cw_grp[:], in_=cw_raw[:].rearrange("p j c -> p c j"))
         cw_q = const.tile([P, C], U32, name="cw_q", align_bytes=64)
         cw_s = const.tile([P, C], U8, name="cw_s", align_bytes=64)
-        nc.vector.quantize_mx(
-            out=cw_q[:].bitcast(E4X4), scales=cw_s[:], in_=cw_grp[:].rearrange("p c j -> p (c j)")
-        )
 
-        ring = const.tile([P, 5 * NCT * RING + RING], F32, name="ring")
-        ring_v = ring[:, 0 : 5 * NCT * RING].rearrange("c (m ct r) -> c m ct r", ct=NCT, r=RING)
+        ring = const.tile([P, 5 * NCT * RS], F32, name="ring")
+        ring_v = ring[:].rearrange("c (m ct r) -> c m ct r", ct=NCT, r=RS)
 
         def ring_cols(m, lo, hi):
-            return ring_v[:, m, :, lo:hi]
+            return ring_v[:, m, :, PAD + lo : PAD + hi]
 
-        nc.vector.memset(ring_cols(2, 0, W), 0.0)
-        nc.vector.memset(ring_cols(4, 0, 1), 0.0)
+        def finish_tables():
+            nc.vector.tensor_copy(out=wrow[:, :, :, PER:WW], in_=wrow[:, :, :, 0:P])
+            nc.vector.quantize_mx(
+                out=cw_q[:].bitcast(E4X4), scales=cw_s[:], in_=cw_grp[:].rearrange("p c j -> p (c j)")
+            )
+            nc.vector.memset(ring_cols(1, 0, W), 0.0)
+            nc.vector.memset(ring_cols(4, -1, 0), 0.0)
 
         nstep = NB * NT
         st = {}
@@ -187,29 +197,29 @@ def tile_lablock_t_kernel(tc, x, w, conv_w, conv_b, grad_out, out):
 
         def copy_g1(si):
             g1 = work.tile([P, C], F32, name="g1", bufs=7)
-            nc.scalar.copy(out=g1[:], in_=st[si]["g1_ps"][:])
+            nc.scalar.mul(out=g1[:], in_=st[si]["g1_ps"][:], mul=-1.0)
             st[si]["g1"] = g1
 
-        def maximum(si):
-            mx = small.tile([P, 1], F32, name="mx")
-            nc.vector.tensor_reduce(out=mx[:], in_=st[si]["at_ps"][:], axis=AX.X, op=ALU.max)
-            st[si]["mx"] = mx
+        def minimum(si):
+            mn = small.tile([P, 1], F32, name="mn")
+            nc.vector.tensor_reduce(out=mn[:], in_=st[si]["at_ps"][:], axis=AX.X, op=ALU.min)
+            st[si]["mn"] = mn
 
         def exponential(si):
             s_ = st[si]
-            nmx = small.tile([P, 1], F32, name="nmx")
-            nc.scalar.mul(out=nmx[:], in_=s_["mx"][:], mul=-1.0)
             ex = work.tile([P, C], F32, name="ex")
             ssum = small.tile([P, 1], F32, name="ssum")
             nc.scalar.activation(
-                out=ex[:], in_=s_["at_ps"][:], func=ACT.Exp, bias=nmx[:], scale=1.0, accum_out=ssum[:]
+                out=ex[:], in_=s_["at_ps"][:], func=ACT.Exp, bias=s_["mn"][:], scale=-1.0, accum_out=ssum[:]
             )
+            nsum = small.tile([P, 1], F32, name="nsum")
+            nc.scalar.mul(out=nsum[:], in_=ssum[:], mul=-1.0)
             s_["ex"] = ex
-            s_["ssum"] = ssum
+            s_["nsum"] = nsum
 
         def one_over_sum(si):
             rs = small.tile([P, 1], F32, name="rs")
-            nc.vector.reciprocal(out=rs[:], in_=st[si]["ssum"][:])
+            nc.vector.reciprocal(out=rs[:], in_=st[si]["nsum"][:])
             st[si]["rs"] = rs
 
         def att_times_g1(si):
@@ -225,24 +235,18 @@ def tile_lablock_t_kernel(tc, x, w, conv_w, conv_b, grad_out, out):
             att_t = work.tile([P, C], F32, name="att_t")
             rr = small.tile([P, 1], F32, name="rr")
             nc.vector.scalar_tensor_tensor(
-                out=att_t[:], in0=s_["ag"][:], scalar=1.0, in1=s_["xt_ps"], op0=ALU.mult, op1=ALU.mult,
+                out=att_t[:], in0=s_["ag"][:], scalar=-1.0, in1=s_["xt_ps"], op0=ALU.mult, op1=ALU.mult,
                 accum_out=rr[:],
             )
             s_["att_t"] = att_t
             s_["rr"] = rr
 
-        def minus_r_over_sum(si):
-            s_ = st[si]
-            nrr = small.tile([P, 1], F32, name="nrr")
-            nc.vector.tensor_scalar(
-                out=nrr[:], in0=s_["rr"][:], scalar1=s_["rs"][:], scalar2=-1.0, op0=ALU.mult, op1=ALU.mult
-            )
-            s_["nrr"] = nrr
-
         def minus_att_times_r(si):
             s_ = st[si]
+            nrr = small.tile([P, 1], F32, name="nrr")
+            nc.scalar.mul(out=nrr[:], in_=s_["rr"][:], mul=s_["rs"][:])
             ar = work.tile([P, C], F32, name="ar")
-            nc.scalar.activation(out=ar[:], in_=s_["ex"][:], func=ACT.Copy, scale=s_["nrr"][:])
+            nc.scalar.activation(out=ar[:], in_=s_["ex"][:], func=ACT.Copy, scale=nrr[:])
             s_["ar"] = ar
 
         def turn_logit_gradient(si):
@@ -251,67 +255,62 @@ def tile_lablock_t_kernel(tc, x, w, conv_w, conv_b, grad_out, out):
             turn(da_ps, [lambda ct, t=t: s_[t][:, ct * P : (ct + 1) * P] for t in ("att_t", "ar")])
             s_["da_ps"] = da_ps
 
-        def weigh(si, m0, m1, q0, q1):
-            bl, col, e0 = tile_of(si)
+        def weigh(si, m0, m1, q0, q1, col):
+            e0 = tile_of(si)[2]
             nm = m1 - m0
             da = st[si]["da_ps"][:].rearrange("c (ct q) -> c ct q", q=P)[:, :, q0:q1]
-            first = (P * si + OFF[m0] + q0) % RING
             if nm == 1:
-                nc.vector.tensor_tensor(
-                    out=ring_cols(m0, first, first + q1 - q0),
-                    in0=da,
-                    in1=wrow[:, m0, :, e0 + q0 : e0 + q1],
-                    op=ALU.mult,
-                )
+                target = ring_cols(m0, col, col + q1 - q0)
+                weights = wrow[:, m0, :, e0 + q0 : e0 + q1]
             else:
-                step = NCT * RING + OFF[m0 + 1] - OFF[m0]
-                base = m0 * NCT * RING + first
-                target = ring[:, base : base + nm * step]
-                target = target.rearrange("c (m s) -> c m s", s=step)[:, :, 0 : NCT * RING]
-                target = target.rearrange("c m (ct r) -> c m ct r", r=RING)[:, :, :, 0:P]
-                nc.vector.tensor_tensor(
-                    out=target,
-                    in0=da.unsqueeze(1).to_broadcast([P, nm, NCT, P]),
-                    in1=wrow[:, m0:m1, :, e0 : e0 + P],
-                    op=ALU.mult,
-                )
+                step = NCT * RS + (OFF[m0 + 1] - OFF[m0] if m0 < NV else 0)
+                base = m0 * NCT * RS + PAD + col
+                target = ring_flat(base, nm, step)[:, :, :, 0 : q1 - q0]
+                weights = wrow[:, m0:m1, :, e0 + q0 : e0 + q1]
+                da = da.unsqueeze(1).to_broadcast([P, nm, NCT, q1 - q0])
+            nc.vector.tensor_tensor(out=target, in0=da, in1=weights, op=ALU.mult)
 
-        def weigh_plan(si):
-            if si % 4 == 0:
-                part_a = [(3, 4, 1, P), (4, 5, 0, P)]
-                part_b = [(1, 3, 0, P), (0, 1, W, P)]
-                if si > 0:
-                    part_a.append((3, 4, 0, 1))
-                if si % NT != 0:
-                    part_b.append((0, 1, 0, W))
-            elif si % 4 == 3:
-                part_a = [(3, 4, 0, P), (4, 5, 0, P - 1)]
-                part_b = [(0, 2, 0, P), (2, 3, 0, P - W)]
-                if si < nstep - 1:
-                    part_a.append((4, 5, P - 1, P))
-                if si % NT != NT - 1:
-                    part_b.append((2, 3, P - W, P))
-            else:
-                part_a = [(3, 5, 0, P)]
-                part_b = [(0, 3, 0, P)]
-            return part_a, part_b
+        def ring_flat(base, nm, step):
+            if step == NCT * RS:
+                m0, col = divmod(base, step)
+                return ring_v[:, m0 : m0 + nm, :, col:RS]
+            taps = ring[:, base : base + nm * step].rearrange("c (m s) -> c m s", s=step)
+            return taps[:, :, 0 : NCT * RS].rearrange("c m (ct r) -> c m ct r", r=RS)
 
         def weigh_part(si, part):
-            if si < nstep:
-                for m0, m1, q0, q1 in weigh_plan(si)[part]:
-                    weigh(si, m0, m1, q0, q1)
+            q = P * si % RING
+            if si < nstep and part == 0:
+                weigh(si, 2, 5, 0, P, q)
+                if q == 0 and si > 0:
+                    weigh(si, 3, 4, 0, 1, RING)
+                if q == RING - P and si < nstep - 1:
+                    weigh(si, 4, 5, P - 1, P, -1)
+            if si < nstep and part == 1:
+                up, down = q - W, q + W
+                if q == 0:
+                    weigh(si, 1, 2, 0, P, down)
+                    weigh(si, 0, 1, W, P, 0)
+                    if si % NT != 0:
+                        weigh(si, 0, 1, 0, W, up + RING)
+                elif q == RING - P:
+                    weigh(si, 0, 1, 0, P, up)
+                    weigh(si, 1, 2, 0, P - W, down)
+                    if si % NT != NT - 1:
+                        weigh(si, 1, 2, P - W, P, 0)
+                else:
+                    weigh(si, 0, 2, 0, P, up)
             if part == 1:
                 if si % NT == 0 and si > 0:
                     nc.vector.memset(ring_cols(0, RING - W, RING), 0.0)
                 if si % NT == NT - 1 and si < nstep - 1:
-                    nc.vector.memset(ring_cols(2, 0, W), 0.0)
+                    nc.vector.memset(ring_cols(1, 0, W), 0.0)
                 if si == nstep:
-                    nc.vector.memset(ring_cols(3, RING - 1, RING), 0.0)
+                    nc.vector.memset(ring_cols(3, RING, RING + 1), 0.0)
 
         def turn_sum(si):
             q = P * si % RING
             sum_ps = psum.tile([P, C], F32, name="sum_ps")
-            turn(sum_ps, [lambda ct, m=m: ring_cols(m, q, q + P)[:, ct, :] for m in range(5)])
+            turn(sum_ps, [lambda ct, m=m, o=o: ring_cols(m, q - o, q - o + P)[:, ct, :] for m, o in enumerate(SHIFT)])
             st[si]["sum_ps"] = sum_ps
 
         def copy_sum(si):
@@ -332,8 +331,8 @@ def tile_lablock_t_kernel(tc, x, w, conv_w, conv_b, grad_out, out):
                 st["osb"] = osb
             q = P * (si % 4)
             osb = st["osb"]
-            nc.scalar.copy(
-                out=osb[:, :, q : q + P], in_=st[si]["out_ps"][:].rearrange("c (ct q) -> c ct q", q=P)
+            nc.scalar.mul(
+                out=osb[:, :, q : q + P], in_=st[si]["out_ps"][:].rearrange("c (ct q) -> c ct q", q=P), mul=-1.0
             )
             if si >= nstep - 4:
                 nc.sync.dma_start(out=o_v[b][:, :, P * a : P * a + P], in_=osb[:, :, q : q + P])
@@ -357,7 +356,7 @@ def tile_lablock_t_kernel(tc, x, w, conv_w, conv_b, grad_out, out):
             if v0:
                 att_times_g1(t0)
             if v1:
-                maximum(t1)
+                minimum(t1)
                 exponential(t1)
             if v0:
                 att_times_t(t0)
@@ -366,7 +365,6 @@ def tile_lablock_t_kernel(tc, x, w, conv_w, conv_b, grad_out, out):
             if 0 <= te <= nstep:
                 weigh_part(te, 0)
             if v0:
-                minus_r_over_sum(t0)
                 minus_att_times_r(t0)
             if 0 <= td < nstep:
                 copy_sum(td)
@@ -388,5 +386,7 @@ def tile_lablock_t_kernel(tc, x, w, conv_w, conv_b, grad_out, out):
             if v3:
                 products(t3, G_TAPS, nc.gpsimd)
                 products(t3, V_TAPS, nc.vector)
+            if i == -3:
+                finish_tables()
             if v2:
                 turn_products(t2)

@@ -23,15 +23,14 @@ PER = KT * W
 WW = PER + P
 TAPS = (1, 2, 0, 3, 4)
 OFF = (-W, W, 0, -1, 1)
-XPAD = 80
+XPAD = 88
 XE = GRP + 2 * XPAD
 RING = 4 * P
 PAD = 4
 RS = RING + 2 * PAD
 SHIFT = (0, 0, 0, -1, 1)
 NV = 2
-G_TAPS = (0, 1, 2)
-V_TAPS = (3, 4)
+G_TAPS = (2, 3, 4)
 FLOPS = 2 * O * C * NB * HW
 
 
@@ -56,8 +55,9 @@ def tile_lablock_t_kernel(tc, x, w, conv_w, conv_b, grad_out, out):
         make_identity(nc, ident_b[:])
 
         wsm = const.tile([P, 5, NCT, 64], BF16, name="wsm")
-        for m in range(5):
-            nc.scalar.dma_start(
+        for m in (2, 3, 4, 0, 1):
+            queue = nc.sync if m < NV else nc.scalar
+            queue.dma_start(
                 out=wsm[:, m, :, 0 : KT * KT], in_=w[TAPS[m]].rearrange("(ct c) r s -> c ct (r s)", c=P)
             )
 
@@ -80,7 +80,7 @@ def tile_lablock_t_kernel(tc, x, w, conv_w, conv_b, grad_out, out):
         load_group(0)
 
         wrow = const.tile([P, 5, NCT, WW], BF16, name="wrow")
-        for m in range(5):
+        for m in (2, 3, 4, 0, 1):
             for ct in range(NCT):
                 rows = wrow[:, m, ct, 0:PER].rearrange("c (r j) -> c r j", j=W)
                 src = wsm[:, m, ct, 0 : KT * KT].rearrange("c (r s) -> c r s", s=KT)
@@ -142,16 +142,25 @@ def tile_lablock_t_kernel(tc, x, w, conv_w, conv_b, grad_out, out):
             pairs[si]["g_q"] = g_q
             pairs[si]["g_s"] = g_s
 
-        def products(si, taps, eng):
+        def products_gpsimd(si):
             bl, col, e0 = tile_of(si)
-            for m in taps:
+            for m in G_TAPS:
                 x0 = XPAD + col + OFF[m]
-                eng.tensor_tensor(
+                nc.gpsimd.tensor_tensor(
                     out=st[si]["prod"][:, m, :, :],
                     in0=bl["xs"][:, :, x0 : x0 + P],
                     in1=wrow[:, m, :, e0 : e0 + P],
                     op=ALU.mult,
                 )
+
+        def products_vector(si):
+            bl, col, e0 = tile_of(si)
+            x0 = XPAD + col + OFF[0]
+            step = OFF[1] - OFF[0]
+            x_up_down = bl["xs"][:, :, x0 : x0 + NV * step].rearrange("c ct (m s) -> c m ct s", s=step)[:, :, :, 0:P]
+            nc.vector.tensor_tensor(
+                out=st[si]["prod"][:, 0:NV, :, :], in0=x_up_down, in1=wrow[:, 0:NV, :, e0 : e0 + P], op=ALU.mult
+            )
 
         def turn(out, pieces):
             for pi, piece in enumerate(pieces):
@@ -168,7 +177,7 @@ def tile_lablock_t_kernel(tc, x, w, conv_w, conv_b, grad_out, out):
         def turn_products(si):
             prod = st[si]["prod"]
             at_ps = psum.tile([P, C], F32, name="at_ps")
-            turn(at_ps, [lambda ct, m=m: prod[:, m, ct, :] for m in V_TAPS + G_TAPS])
+            turn(at_ps, [lambda ct, m=m: prod[:, m, ct, :] for m in range(5)])
             st[si]["at_ps"] = at_ps
 
         def turn_x_and_multiply_pair(si):
@@ -233,18 +242,18 @@ def tile_lablock_t_kernel(tc, x, w, conv_w, conv_b, grad_out, out):
         def att_times_t(si):
             s_ = st[si]
             att_t = work.tile([P, C], F32, name="att_t")
-            rr = small.tile([P, 1], F32, name="rr")
             nc.vector.scalar_tensor_tensor(
-                out=att_t[:], in0=s_["ag"][:], scalar=-1.0, in1=s_["xt_ps"], op0=ALU.mult, op1=ALU.mult,
-                accum_out=rr[:],
+                out=att_t[:], in0=s_["ag"][:], scalar=-1.0, in1=s_["xt_ps"], op0=ALU.mult, op1=ALU.mult
             )
             s_["att_t"] = att_t
-            s_["rr"] = rr
 
         def minus_att_times_r(si):
             s_ = st[si]
+            scaled = work.tile([P, C], BF16, name="scaled", bufs=2)
             nrr = small.tile([P, 1], F32, name="nrr")
-            nc.scalar.mul(out=nrr[:], in_=s_["rr"][:], mul=s_["rs"][:])
+            nc.scalar.activation(
+                out=scaled[:], in_=s_["att_t"][:], func=ACT.Copy, scale=s_["rs"][:], accum_out=nrr[:]
+            )
             ar = work.tile([P, C], F32, name="ar")
             nc.scalar.activation(out=ar[:], in_=s_["ex"][:], func=ACT.Copy, scale=nrr[:])
             s_["ar"] = ar
@@ -384,8 +393,8 @@ def tile_lablock_t_kernel(tc, x, w, conv_w, conv_b, grad_out, out):
             if v3 and t3 % 2 == 0:
                 regroup_pair(t3)
             if v3:
-                products(t3, G_TAPS, nc.gpsimd)
-                products(t3, V_TAPS, nc.vector)
+                products_gpsimd(t3)
+                products_vector(t3)
             if i == -3:
                 finish_tables()
             if v2:

from contextlib import ExitStack

import concourse.mybir as mybir
from concourse.masks import make_identity

F32 = mybir.dt.float32
BF16 = mybir.dt.bfloat16
U32 = mybir.dt.uint32
U8 = mybir.dt.uint8
E4X4 = mybir.dt.float8_e4m3fn_x4
E5X4 = mybir.dt.float8_e5m2_x4
ALU = mybir.AluOpType
ACT = mybir.ActivationFunctionType
AX = mybir.AxisListType

NB, C, O, H, W, KT = 2, 512, 512, 64, 72, 7
HW = H * W
P = 128
NCT = C // P
NT = HW // P
GRP = 4 * P
PER = KT * W
WW = PER + P
TAPS = (1, 2, 0, 3, 4)
OFF = (-W, W, 0, -1, 1)
XPAD = 88
XE = GRP + 2 * XPAD
RING = 4 * P
PAD = 4
RS = RING + 2 * PAD
SHIFT = (0, 0, 0, -1, 1)
NV = 2
G_TAPS = (2, 3, 4)
FLOPS = 2 * O * C * NB * HW


def tile_lablock_t_kernel(tc, x, w, conv_w, conv_b, grad_out, out):
    nc = tc.nc
    x_v = x.rearrange("b (ct c) h w -> b c ct (h w)", c=P)
    g_v = grad_out.rearrange("b (p j) h w -> b p j (h w)", j=4)
    o_v = out.rearrange("b (ct c) h w -> b c ct (h w)", c=P)

    with ExitStack() as ctx:
        const = ctx.enter_context(tc.tile_pool(name="const", bufs=1))
        load = ctx.enter_context(tc.tile_pool(name="load", bufs=3))
        quant = ctx.enter_context(tc.tile_pool(name="quant", bufs=3))
        work = ctx.enter_context(tc.tile_pool(name="work", bufs=3))
        small = ctx.enter_context(tc.tile_pool(name="small", bufs=4))
        store = ctx.enter_context(tc.tile_pool(name="store", bufs=2))
        psum = ctx.enter_context(tc.psum_pool(name="psum", bufs=1))

        ident_f = const.tile([P, P], F32, name="ident_f")
        make_identity(nc, ident_f[:])
        ident_b = const.tile([P, P], BF16, name="ident_b")
        make_identity(nc, ident_b[:])

        wsm = const.tile([P, 5, NCT, 64], BF16, name="wsm")
        for m in (2, 3, 4, 0, 1):
            queue = nc.sync if m < NV else nc.scalar
            queue.dma_start(
                out=wsm[:, m, :, 0 : KT * KT], in_=w[TAPS[m]].rearrange("(ct c) r s -> c ct (r s)", c=P)
            )

        blk = {}

        def load_group(gi):
            b, k = divmod(gi, NT // 4)
            xs = load.tile([P, NCT, XE], BF16, name="xs")
            lo = GRP * k - XPAD
            clo, chi = max(lo, 0), min(lo + XE, HW)
            if clo > lo:
                nc.gpsimd.memset(xs[:, :, 0 : clo - lo], 0.0)
            if chi < lo + XE:
                nc.gpsimd.memset(xs[:, :, chi - lo : XE], 0.0)
            nc.sync.dma_start(out=xs[:, :, clo - lo : chi - lo], in_=x_v[b][:, :, clo:chi])
            g_raw = load.tile([P, 4, GRP], BF16, name="g_raw")
            nc.sync.dma_start(out=g_raw[:], in_=g_v[b][:, :, GRP * k : GRP * k + GRP])
            blk[gi] = {"xs": xs, "g_raw": g_raw}

        load_group(0)

        wrow = const.tile([P, 5, NCT, WW], BF16, name="wrow")
        for m in (2, 3, 4, 0, 1):
            for ct in range(NCT):
                rows = wrow[:, m, ct, 0:PER].rearrange("c (r j) -> c r j", j=W)
                src = wsm[:, m, ct, 0 : KT * KT].rearrange("c (r s) -> c r s", s=KT)
                nc.vector.tensor_scalar(
                    out=rows[:, :, 0:70].rearrange("c r (jb s) -> c r jb s", s=KT),
                    in0=src.unsqueeze(2).to_broadcast([P, KT, 10, KT]),
                    scalar1=-1.0,
                    scalar2=None,
                    op0=ALU.mult,
                )
                nc.vector.tensor_scalar(
                    out=rows[:, :, 70:72], in0=src[:, :, 0:2], scalar1=-1.0, scalar2=None, op0=ALU.mult
                )
        nc.vector.memset(wrow[:, 3, :, 0:PER:W], 0.0)
        nc.vector.memset(wrow[:, 4, :, W - 1 : PER : W], 0.0)

        cw_raw = const.tile([P, 4, C], BF16, name="cw_raw")
        nc.sync.dma_start(out=cw_raw[:], in_=conv_w.rearrange("(p j) c -> p j c", j=4))
        cw_grp = const.tile([P, C, 4], BF16, name="cw_grp", align_bytes=64)
        nc.scalar.copy(out=cw_grp[:], in_=cw_raw[:].rearrange("p j c -> p c j"))
        cw_q = const.tile([P, C], U32, name="cw_q", align_bytes=64)
        cw_s = const.tile([P, C], U8, name="cw_s", align_bytes=64)

        ring = const.tile([P, 5 * NCT * RS], F32, name="ring")
        ring_v = ring[:].rearrange("c (m ct r) -> c m ct r", ct=NCT, r=RS)

        def ring_cols(m, lo, hi):
            return ring_v[:, m, :, PAD + lo : PAD + hi]

        def finish_tables():
            nc.vector.tensor_copy(out=wrow[:, :, :, PER:WW], in_=wrow[:, :, :, 0:P])
            nc.vector.quantize_mx(
                out=cw_q[:].bitcast(E4X4), scales=cw_s[:], in_=cw_grp[:].rearrange("p c j -> p (c j)")
            )
            nc.vector.memset(ring_cols(1, 0, W), 0.0)
            nc.vector.memset(ring_cols(4, -1, 0), 0.0)

        nstep = NB * NT
        st = {}

        def tile_of(si):
            b, a = divmod(si, NT)
            return blk[si // 4], P * (si % 4), (P * a) % PER

        pairs = {}

        def regroup_pair(si):
            bl, col, e0 = tile_of(si)
            g_grp = quant.tile([P, 2 * P, 4], BF16, name="g_grp", align_bytes=64)
            nc.scalar.copy(out=g_grp[:], in_=bl["g_raw"][:, :, col : col + 2 * P].rearrange("p j q -> p q j"))
            pairs[si] = {"g_grp": g_grp}

        def quantise_pair(si):
            g_q = quant.tile([P, 2 * P], U32, name="g_q", align_bytes=64)
            g_s = quant.tile([P, 2 * P], U8, name="g_s", align_bytes=64)
            nc.vector.quantize_mx(
                out=g_q[:].bitcast(E5X4), scales=g_s[:], in_=pairs[si]["g_grp"][:].rearrange("p q j -> p (q j)")
            )
            pairs[si]["g_q"] = g_q
            pairs[si]["g_s"] = g_s

        def products_gpsimd(si):
            bl, col, e0 = tile_of(si)
            for m in G_TAPS:
                x0 = XPAD + col + OFF[m]
                nc.gpsimd.tensor_tensor(
                    out=st[si]["prod"][:, m, :, :],
                    in0=bl["xs"][:, :, x0 : x0 + P],
                    in1=wrow[:, m, :, e0 : e0 + P],
                    op=ALU.mult,
                )

        def products_vector(si):
            bl, col, e0 = tile_of(si)
            x0 = XPAD + col + OFF[0]
            step = OFF[1] - OFF[0]
            x_up_down = bl["xs"][:, :, x0 : x0 + NV * step].rearrange("c ct (m s) -> c m ct s", s=step)[:, :, :, 0:P]
            nc.vector.tensor_tensor(
                out=st[si]["prod"][:, 0:NV, :, :], in0=x_up_down, in1=wrow[:, 0:NV, :, e0 : e0 + P], op=ALU.mult
            )

        def turn(out, pieces):
            for pi, piece in enumerate(pieces):
                for ct in range(NCT):
                    nc.tensor.matmul(
                        out=out[:, ct * P : (ct + 1) * P],
                        lhsT=piece(ct),
                        rhs=ident_f[:],
                        is_transpose=True,
                        start=(pi == 0 and ct == 0),
                        stop=(pi == len(pieces) - 1 and ct == NCT - 1),
                    )

        def turn_products(si):
            prod = st[si]["prod"]
            at_ps = psum.tile([P, C], F32, name="at_ps")
            turn(at_ps, [lambda ct, m=m: prod[:, m, ct, :] for m in range(5)])
            st[si]["at_ps"] = at_ps

        def turn_x_and_multiply_pair(si):
            xt_ps = psum.tile([P, 2, C], BF16, name="xt_ps")
            for u in range(2):
                bl, col, e0 = tile_of(si + u)
                for ct in range(NCT):
                    nc.tensor.transpose(
                        out=xt_ps[:, u, ct * P : (ct + 1) * P],
                        in_=bl["xs"][:, ct, XPAD + col : XPAD + col + P],
                        identity=ident_b[:],
                    )
                st[si + u]["xt_ps"] = xt_ps[:, u, :]
            for u in range(2):
                g1_ps = psum.tile([P, C], F32, name="g1_ps", bufs=2)
                nc.tensor.matmul_mx(
                    out=g1_ps[:],
                    lhsT=pairs[si]["g_q"][:, u * P : (u + 1) * P].bitcast(E5X4),
                    lhsT_scale=pairs[si]["g_s"][:, u * P : (u + 1) * P],
                    rhs=cw_q[:].bitcast(E4X4),
                    rhs_scale=cw_s[:],
                    start=True,
                    stop=True,
                )
                st[si + u]["g1_ps"] = g1_ps

        def copy_g1(si):
            g1 = work.tile([P, C], F32, name="g1", bufs=7)
            nc.scalar.mul(out=g1[:], in_=st[si]["g1_ps"][:], mul=-1.0)
            st[si]["g1"] = g1

        def minimum(si):
            mn = small.tile([P, 1], F32, name="mn")
            nc.vector.tensor_reduce(out=mn[:], in_=st[si]["at_ps"][:], axis=AX.X, op=ALU.min)
            st[si]["mn"] = mn

        def exponential(si):
            s_ = st[si]
            ex = work.tile([P, C], F32, name="ex")
            ssum = small.tile([P, 1], F32, name="ssum")
            nc.scalar.activation(
                out=ex[:], in_=s_["at_ps"][:], func=ACT.Exp, bias=s_["mn"][:], scale=-1.0, accum_out=ssum[:]
            )
            nsum = small.tile([P, 1], F32, name="nsum")
            nc.scalar.mul(out=nsum[:], in_=ssum[:], mul=-1.0)
            s_["ex"] = ex
            s_["nsum"] = nsum

        def one_over_sum(si):
            rs = small.tile([P, 1], F32, name="rs")
            nc.vector.reciprocal(out=rs[:], in_=st[si]["nsum"][:])
            st[si]["rs"] = rs

        def att_times_g1(si):
            s_ = st[si]
            ag = work.tile([P, C], F32, name="ag", bufs=6)
            nc.vector.scalar_tensor_tensor(
                out=ag[:], in0=s_["ex"][:], scalar=s_["rs"][:], in1=s_["g1_ps"][:], op0=ALU.mult, op1=ALU.mult
            )
            s_["ag"] = ag

        def att_times_t(si):
            s_ = st[si]
            att_t = work.tile([P, C], F32, name="att_t")
            nc.vector.scalar_tensor_tensor(
                out=att_t[:], in0=s_["ag"][:], scalar=-1.0, in1=s_["xt_ps"], op0=ALU.mult, op1=ALU.mult
            )
            s_["att_t"] = att_t

        def minus_att_times_r(si):
            s_ = st[si]
            scaled = work.tile([P, C], BF16, name="scaled", bufs=2)
            nrr = small.tile([P, 1], F32, name="nrr")
            nc.scalar.activation(
                out=scaled[:], in_=s_["att_t"][:], func=ACT.Copy, scale=s_["rs"][:], accum_out=nrr[:]
            )
            ar = work.tile([P, C], F32, name="ar")
            nc.scalar.activation(out=ar[:], in_=s_["ex"][:], func=ACT.Copy, scale=nrr[:])
            s_["ar"] = ar

        def turn_logit_gradient(si):
            s_ = st[si]
            da_ps = psum.tile([P, C], F32, name="da_ps", bufs=2)
            turn(da_ps, [lambda ct, t=t: s_[t][:, ct * P : (ct + 1) * P] for t in ("att_t", "ar")])
            s_["da_ps"] = da_ps

        def weigh(si, m0, m1, q0, q1, col):
            e0 = tile_of(si)[2]
            nm = m1 - m0
            da = st[si]["da_ps"][:].rearrange("c (ct q) -> c ct q", q=P)[:, :, q0:q1]
            if nm == 1:
                target = ring_cols(m0, col, col + q1 - q0)
                weights = wrow[:, m0, :, e0 + q0 : e0 + q1]
            else:
                step = NCT * RS + (OFF[m0 + 1] - OFF[m0] if m0 < NV else 0)
                base = m0 * NCT * RS + PAD + col
                target = ring_flat(base, nm, step)[:, :, :, 0 : q1 - q0]
                weights = wrow[:, m0:m1, :, e0 + q0 : e0 + q1]
                da = da.unsqueeze(1).to_broadcast([P, nm, NCT, q1 - q0])
            nc.vector.tensor_tensor(out=target, in0=da, in1=weights, op=ALU.mult)

        def ring_flat(base, nm, step):
            if step == NCT * RS:
                m0, col = divmod(base, step)
                return ring_v[:, m0 : m0 + nm, :, col:RS]
            taps = ring[:, base : base + nm * step].rearrange("c (m s) -> c m s", s=step)
            return taps[:, :, 0 : NCT * RS].rearrange("c m (ct r) -> c m ct r", r=RS)

        def weigh_part(si, part):
            q = P * si % RING
            if si < nstep and part == 0:
                weigh(si, 2, 5, 0, P, q)
                if q == 0 and si > 0:
                    weigh(si, 3, 4, 0, 1, RING)
                if q == RING - P and si < nstep - 1:
                    weigh(si, 4, 5, P - 1, P, -1)
            if si < nstep and part == 1:
                up, down = q - W, q + W
                if q == 0:
                    weigh(si, 1, 2, 0, P, down)
                    weigh(si, 0, 1, W, P, 0)
                    if si % NT != 0:
                        weigh(si, 0, 1, 0, W, up + RING)
                elif q == RING - P:
                    weigh(si, 0, 1, 0, P, up)
                    weigh(si, 1, 2, 0, P - W, down)
                    if si % NT != NT - 1:
                        weigh(si, 1, 2, P - W, P, 0)
                else:
                    weigh(si, 0, 2, 0, P, up)
            if part == 1:
                if si % NT == 0 and si > 0:
                    nc.vector.memset(ring_cols(0, RING - W, RING), 0.0)
                if si % NT == NT - 1 and si < nstep - 1:
                    nc.vector.memset(ring_cols(1, 0, W), 0.0)
                if si == nstep:
                    nc.vector.memset(ring_cols(3, RING, RING + 1), 0.0)

        def turn_sum(si):
            q = P * si % RING
            sum_ps = psum.tile([P, C], F32, name="sum_ps")
            turn(sum_ps, [lambda ct, m=m, o=o: ring_cols(m, q - o, q - o + P)[:, ct, :] for m, o in enumerate(SHIFT)])
            st[si]["sum_ps"] = sum_ps

        def copy_sum(si):
            total = work.tile([P, C], F32, name="total")
            nc.scalar.copy(out=total[:], in_=st[si]["sum_ps"][:])
            st[si]["total"] = total

        def turn_out(si):
            s_ = st[si]
            out_ps = psum.tile([P, C], F32, name="out_ps")
            turn(out_ps, [lambda ct, t=t: s_[t][:, ct * P : (ct + 1) * P] for t in ("g1", "ag", "total")])
            s_["out_ps"] = out_ps

        def copy_out(si):
            b, a = divmod(si, NT)
            if si % 4 == 0:
                osb = store.tile([P, NCT, GRP], F32, name="osb")
                st["osb"] = osb
            q = P * (si % 4)
            osb = st["osb"]
            nc.scalar.mul(
                out=osb[:, :, q : q + P], in_=st[si]["out_ps"][:].rearrange("c (ct q) -> c ct q", q=P), mul=-1.0
            )
            if si >= nstep - 4:
                nc.sync.dma_start(out=o_v[b][:, :, P * a : P * a + P], in_=osb[:, :, q : q + P])
            elif si % 4 == 3:
                nc.sync.dma_start(out=o_v[b][:, :, P * (a - 3) : P * (a + 1)], in_=osb[:])

        ctx.enter_context(tc.manual_schedule())
        for i in range(-3, nstep + 4):
            t0, t1, t2, t3 = i, i + 1, i + 2, i + 3
            te, td, to = i - 1, i - 3, i - 4
            v0 = 0 <= t0 < nstep
            v1 = 0 <= t1 < nstep
            v2 = 0 <= t2 < nstep
            v3 = t3 < nstep
            if (i + 7) % 4 == 0 and 1 <= (i + 7) // 4 < nstep // 4:
                load_group((i + 7) // 4)
            if v3:
                st[t3] = {"prod": work.tile([P, 5, NCT, P], F32, name="prod", bufs=2)}
            if 0 <= te < nstep:
                turn_logit_gradient(te)
            if v0:
                att_times_g1(t0)
            if v1:
                minimum(t1)
                exponential(t1)
            if v0:
                att_times_t(t0)
            if 0 <= td < nstep:
                turn_sum(td)
            if 0 <= te <= nstep:
                weigh_part(te, 0)
            if v0:
                minus_att_times_r(t0)
            if 0 <= td < nstep:
                copy_sum(td)
            if 0 <= to < nstep:
                turn_out(to)
                copy_out(to)
            if 0 <= te <= nstep:
                weigh_part(te, 1)
            if v1 and t1 % 2 == 0:
                turn_x_and_multiply_pair(t1)
                copy_g1(t1)
                copy_g1(t1 + 1)
            if v1:
                one_over_sum(t1)
            if v2 and t2 % 2 == 0:
                quantise_pair(t2)
            if v3 and t3 % 2 == 0:
                regroup_pair(t3)
            if v3:
                products_gpsimd(t3)
                products_vector(t3)
            if i == -3:
                finish_tables()
            if v2:
                turn_products(t2)
